import numpy as np
import ml_dtypes


def mxq(x, axis, fmt="e4m3"):
    dtype, down = {"e4m3": (ml_dtypes.float8_e4m3fn, 7), "e5m2": (ml_dtypes.float8_e5m2, 14)}[fmt]
    v = np.moveaxis(np.asarray(x, np.float32).astype(ml_dtypes.bfloat16).astype(np.float64), axis, -1)
    blocks = v.reshape(v.shape[:-1] + (-1, 32))
    amax = np.abs(blocks).max(-1, keepdims=True)
    byte = np.maximum(np.where(amax > 0, np.frexp(amax)[1] - 1 + 127, 0) - down, 1)
    scale = np.exp2(byte - 127.0)
    codes = (blocks / scale).astype(np.float32).astype(dtype).astype(np.float64)
    return np.moveaxis((codes * scale).reshape(v.shape), -1, axis)


WIDE = False


def mx_kscale(k):
    if not WIDE:
        return np.ones(k)
    levels = np.array([10, -10, 5, -5, 0])
    a = np.random.permutation(np.resize(levels, k // 512 * 4)).reshape(k // 512, 4)
    idx = np.arange(k)
    return np.exp2(a[idx // 512, idx % 128 // 32])


BF16 = ml_dtypes.bfloat16


def bf(x):
    return np.asarray(x, np.float32).astype(BF16)


def f64(x):
    return np.asarray(x).astype(np.float64)


E2M1 = np.array([0.0, 0.5, 1.0, 1.5, 2.0, 3.0, 4.0, 6.0, -0.0, -0.5, -1.0, -1.5, -2.0, -3.0, -4.0, -6.0])


def pack_weight(w, fmt):
    k, n = w.shape
    w = f64(bf(w)).reshape(k // 32, 32, n)
    amax = np.abs(w).max(1)
    if fmt == "e4m3":
        byte = np.frexp(amax)[1] - 1 + 127 - 7
    else:
        mant, ex = np.frexp(amax / 6.0)
        byte = np.where(mant > 0.5, ex, ex - 1) + 127
    byte = np.clip(np.where(amax > 0, byte, 1), 1, 254)
    scaled = (w * np.exp2(127.0 - byte)[:, None, :]).reshape(k, n).astype(np.float32)
    by_word = np.ascontiguousarray(scaled.reshape(k // 512, 128, 4, n).transpose(0, 1, 3, 2))
    if fmt == "e4m3":
        words = by_word.astype(ml_dtypes.float8_e4m3fn).view(np.uint8)
    else:
        c = by_word.astype(ml_dtypes.float4_e2m1fn).view(np.uint8) & 0xF
        words = c[..., 0::2] | (c[..., 1::2] << 4)
    return np.ascontiguousarray(words), np.ascontiguousarray(byte.astype(np.uint8).reshape(k // 512, 16, n))


def unpack_weight(words, scales, fmt):
    g, p, n, _ = words.shape
    if fmt == "e4m3":
        vals = np.ascontiguousarray(words).view(ml_dtypes.float8_e4m3fn).astype(np.float64)
    else:
        nib = np.empty((g, p, n, 4), np.uint8)
        nib[..., 0::2] = words & 0xF
        nib[..., 1::2] = words >> 4
        vals = E2M1[nib]
    vals = vals * np.repeat(np.exp2(scales.astype(np.float64) - 127.0), 8, axis=1)[..., None]
    return vals.transpose(0, 1, 3, 2).reshape(g * 512, n)


B, D, HID, G0, RIN, NR = 256, 1024, 2048, 512, 256, 5
EPS = 1e-05
W2S = 0.02


def silu(v):
    return v / (1.0 + np.exp(-v))


def setup_inputs():
    t = mx_kscale(HID)
    xr = bf(np.random.standard_normal((B, NR, RIN)))
    w1_r = bf(np.random.standard_normal((NR, HID, RIN)) / np.sqrt(RIN))
    w3_r = bf(np.random.standard_normal((NR, HID, RIN)) / np.sqrt(RIN) * t[None, :, None])
    w2 = np.random.standard_normal((NR, D, HID)) * W2S / np.sqrt(HID) / t
    cat = np.ascontiguousarray(w2.swapaxes(1, 2)).reshape(-1, D)
    w2_r_words, w2_r_scales = pack_weight(cat, "e4m3")
    norm_w = bf(1.0 + 0.1 * np.random.standard_normal(D))
    norm_b = bf(0.1 * np.random.standard_normal(D))
    term_embed_r = bf(np.random.standard_normal((NR, D)))
    return {"xr": xr,
            "w1_r": w1_r,
            "w3_r": w3_r,
            "w2_r_words": w2_r_words,
            "w2_r_scales": w2_r_scales,
            "norm_w": norm_w,
            "norm_b": norm_b,
            "term_embed_r": term_embed_r}


def reference(xr, w1_r, w3_r, w2_r_words, w2_r_scales, norm_w, norm_b, term_embed_r):
    xg = f64(xr).transpose(1, 0, 2)
    gate = silu(xg @ f64(w1_r).transpose(0, 2, 1))
    val = xg @ f64(w3_r).transpose(0, 2, 1)
    h = gate * val
    tok = (mxq(h, 2, "e4m3") @ unpack_weight(w2_r_words, w2_r_scales, "e4m3").reshape(NR, HID, D)).transpose(1, 0, 2)
    rms = np.sqrt(np.mean(tok * tok, axis=-1, keepdims=True) + EPS)
    return (tok / rms) * f64(norm_w) + f64(norm_b) + f64(term_embed_r)[None, :, :]

@@ -1,0 +1,293 @@
+from contextlib import ExitStack
+
+import concourse.mybir as mybir
+from concourse.masks import make_identity
+
+F32 = mybir.dt.float32
+BF16 = mybir.dt.bfloat16
+I32 = mybir.dt.int32
+U32 = mybir.dt.uint32
+U8 = mybir.dt.uint8
+FP8X4 = mybir.dt.float8_e4m3fn_x4
+ACT = mybir.ActivationFunctionType
+ALU = mybir.AluOpType
+
+P = 128
+PACK = 4
+BATCH = 256
+GROUPS = 5
+RIN = 256
+HID = 2048
+DOUT = 1024
+EPS = 1e-05
+
+K_PASS = P * PACK
+CHUNKS = HID // K_PASS
+N_CHUNKS = GROUPS * CHUNKS
+UNITS_PER_CHUNK = 2
+UNITS_PER_GROUP = CHUNKS * UNITS_PER_CHUNK
+N_UNITS = GROUPS * UNITS_PER_GROUP
+T_UNIT = PACK // UNITS_PER_CHUNK
+B_TILES = BATCH // P
+BANK = 512
+N_HALVES = DOUT // BANK
+
+LOOK = 3
+RAW_BUFS = 8
+W2_BUFS = 2
+
+FLOPS = 2 * BATCH * GROUPS * (2 * RIN * HID + HID * DOUT)
+
+
+def tile_observationembeddingv2_pb_e_kernel(
+    tc, xr, w1_r, w3_r, w2_r_words, w2_r_scales, norm_w, norm_b, term_embed_r, out
+):
+    nc = tc.nc
+    with ExitStack() as ctx:
+        const = ctx.enter_context(tc.tile_pool(name="const", bufs=1))
+        raw_pool = ctx.enter_context(tc.tile_pool(name="raw", bufs=RAW_BUFS))
+        w2_pool = ctx.enter_context(tc.tile_pool(name="w2", bufs=W2_BUFS))
+        wt_pool = ctx.enter_context(tc.tile_pool(name="wt", bufs=LOOK + 1))
+        h_pool = ctx.enter_context(tc.tile_pool(name="h", bufs=3))
+        q_pool = ctx.enter_context(tc.tile_pool(name="q", bufs=2))
+        e_pool = ctx.enter_context(tc.tile_pool(name="e", bufs=2))
+        psum = ctx.enter_context(tc.psum_pool(name="psum", bufs=2))
+        ctx.enter_context(tc.manual_schedule())
+
+        ident = const.tile([P, P], F32, name="ident")
+        make_identity(nc, ident[:])
+        neg_half = const.tile([P, 1], F32, name="neg_half")
+        nc.gpsimd.memset(neg_half[:], -0.5)
+
+        rows = const.tile([P, DOUT], BF16, name="rows")
+        nc.vector.memset(rows[:], 0.0)
+        w2_planes = const.tile([P, GROUPS, DOUT], U8, name="w2_planes", align_bytes=64)
+        nc.vector.memset(w2_planes[:].bitcast(I32), 0)
+        nc.scalar.dma_start(out=rows[0:1, :], in_=norm_w.unsqueeze(0))
+        nc.scalar.dma_start(out=rows[1:2, :], in_=norm_b.unsqueeze(0))
+        nc.scalar.dma_start(out=rows[2 : 2 + GROUPS, :], in_=term_embed_r)
+        warm = const.tile([P, 1], F32, name="warm")
+        nc.scalar.activation(out=warm[:], in_=neg_half[:], func=ACT.Silu)
+
+        ident_bf = const.tile([P, P], BF16, name="ident_bf")
+        nc.vector.tensor_copy(out=ident_bf[:], in_=ident[:])
+        pick_bias = const.tile([P, GROUPS], BF16, name="pick_bias")
+        nc.vector.tensor_tensor(
+            out=pick_bias[:],
+            in0=ident_bf[:, 1:2].to_broadcast([P, GROUPS]),
+            in1=ident_bf[:, 2 : 2 + GROUPS],
+            op=ALU.add,
+        )
+
+        x_raw = const.tile([P, B_TILES, GROUPS * RIN], BF16, name="x_raw")
+        nc.sync.dma_start(out=x_raw[:], in_=xr.rearrange("(j p) g k -> p j (g k)", p=P))
+        x_words = x_raw[:].bitcast(F32)
+        xT = const.tile([P, GROUPS, BATCH], F32, name="xT")
+        xT_halves = xT[:].bitcast(BF16).rearrange("q g (b e) -> q g b e", e=2)
+        gain = const.tile([P, DOUT], F32, name="gain")
+        bias = const.tile([P, GROUPS, DOUT], F32, name="bias")
+
+        raw = {}
+        w2_words = {}
+        weights_t = {}
+        codes = {}
+        planes = {}
+        grouped = {}
+        silu_sb = {}
+        tok_ps = {}
+        rstd = {}
+
+        def load_chunk(k):
+            g, c = divmod(k, CHUNKS)
+            raw[k] = raw_pool.tile([P, 2, PACK, RIN], BF16, name="raw")
+            for i, w in enumerate((w1_r, w3_r)):
+                nc.sync.dma_start(
+                    out=raw[k][:, i].rearrange("p t k -> p (t k)"),
+                    in_=w[g, c * K_PASS : (c + 1) * K_PASS, :].rearrange(
+                        "(p t) k -> p (t k)", t=PACK
+                    ),
+                )
+
+        def load_w2(g):
+            for quad in range(4):
+                nc.sync.dma_start(
+                    out=w2_planes[32 * quad : 32 * quad + 16, g, :].bitcast(I32),
+                    in_=w2_r_scales[
+                        CHUNKS * g : CHUNKS * (g + 1), 4 * quad : 4 * quad + 4, :
+                    ].bitcast(I32),
+                )
+            w2_words[g] = w2_pool.tile([P, CHUNKS, DOUT], U32, name="w2_words", align_bytes=64)
+            nc.sync.dma_start(
+                out=w2_words[g][:].bitcast(I32),
+                in_=w2_r_words[CHUNKS * g : CHUNKS * (g + 1)]
+                .rearrange("c p n t -> p c (n t)")
+                .bitcast(I32),
+            )
+
+        def spread_row(pick, dest):
+            for nh in range(N_HALVES):
+                cols = slice(nh * BANK, (nh + 1) * BANK)
+                spread_ps = psum.tile([P, BANK], F32, name="spread_ps", tag="av", bufs=4)
+                nc.tensor.matmul(
+                    out=spread_ps[:],
+                    lhsT=pick.to_broadcast([P, P]),
+                    rhs=rows[:, cols],
+                    start=True,
+                    stop=True,
+                )
+                nc.scalar.copy(out=dest[:, cols], in_=spread_ps[:])
+
+        def prepare_group(g):
+            xt_ps = psum.tile([P, B_TILES, P], F32, name="xt_ps", tag="tr", bufs=2)
+            for j in range(B_TILES):
+                nc.tensor.transpose(
+                    xt_ps[:, j, :], x_words[:, j, g * P : (g + 1) * P], ident[:]
+                )
+            nc.scalar.copy(out=xT[:, g, :], in_=xt_ps[:].rearrange("q j b -> q (j b)"))
+            spread_row(pick_bias[:, g : g + 1], bias[:, g, :])
+
+        def transpose_weights(u):
+            k, half = divmod(u, UNITS_PER_CHUNK)
+            raw_words = raw[k][:].bitcast(F32)
+            wt_ps = psum.tile([P, 2 * T_UNIT, P], F32, name="wt_ps", tag="tr", bufs=2)
+            for i in range(2):
+                for tl in range(T_UNIT):
+                    nc.tensor.transpose(
+                        wt_ps[:, i * T_UNIT + tl, :],
+                        raw_words[:, i, half * T_UNIT + tl, :],
+                        ident[:],
+                    )
+            weights_t[u] = wt_pool.tile([P, 2 * T_UNIT, P], F32, name="weights_t")
+            nc.scalar.copy(out=weights_t[u][:], in_=wt_ps[:])
+            if half == UNITS_PER_CHUNK - 1 and k + RAW_BUFS < N_CHUNKS:
+                load_chunk(k + RAW_BUFS)
+
+        def project(u, i):
+            g = u // UNITS_PER_GROUP
+            halves = weights_t[u][:].bitcast(BF16).rearrange("q s (m e) -> q s m e", e=2)
+            acc = psum.tile([P, T_UNIT, BATCH], F32, name="acc", tag="av", bufs=4)
+            for tl in range(T_UNIT):
+                for e in range(2):
+                    nc.tensor.matmul(
+                        out=acc[:, tl, :],
+                        lhsT=halves[:, i * T_UNIT + tl, :, e],
+                        rhs=xT_halves[:, g, :, e],
+                        start=(e == 0),
+                        stop=(e == 1),
+                    )
+            return acc
+
+        def gate(u):
+            gate_ps = project(u, 0)
+            silu_sb[u] = h_pool.tile([P, T_UNIT, BATCH], F32, name="silu_sb")
+            nc.scalar.activation(out=silu_sb[u][:], in_=gate_ps[:], func=ACT.Silu)
+
+        def value_and_product(u):
+            k, half = divmod(u, UNITS_PER_CHUNK)
+            value_ps = project(u, 1)
+            if half == 0:
+                grouped[k] = h_pool.tile([P, BATCH, PACK], BF16, name="grouped", align_bytes=64)
+            nc.vector.tensor_tensor(
+                out=grouped[k][:, :, half * T_UNIT : (half + 1) * T_UNIT],
+                in0=value_ps[:].rearrange("p t b -> p b t"),
+                in1=silu_sb[u][:].rearrange("p t b -> p b t"),
+                op=ALU.mult,
+            )
+
+        def quantise(k):
+            g, c = divmod(k, CHUNKS)
+            if c == 0:
+                codes[g] = q_pool.tile([P, CHUNKS, BATCH], U32, name="codes", align_bytes=64)
+                planes[g] = q_pool.tile([P, CHUNKS, BATCH], U8, name="planes", align_bytes=64)
+            nc.vector.quantize_mx(
+                out=codes[g][:, c, :].bitcast(FP8X4),
+                scales=planes[g][:, c, :],
+                in_=grouped[k][:].rearrange("p b t -> p (b t)"),
+            )
+
+        def down_project(g, j):
+            rows_b = slice(j * P, (j + 1) * P)
+            sumsq = e_pool.tile([P, N_HALVES], F32, name="sumsq")
+            squares = e_pool.tile([P, N_HALVES, BANK], BF16, name="squares")
+            for nh in range(N_HALVES):
+                cols = slice(nh * BANK, (nh + 1) * BANK)
+                tok_ps[nh] = psum.tile([P, BANK], F32, name="tok_ps", tag="tok", bufs=2)
+                for c in range(CHUNKS):
+                    nc.tensor.matmul_mx(
+                        out=tok_ps[nh][:],
+                        lhsT=codes[g][:, c, rows_b].bitcast(FP8X4),
+                        lhsT_scale=planes[g][:, c, rows_b],
+                        rhs=w2_words[g][:, c, cols].bitcast(FP8X4),
+                        rhs_scale=w2_planes[4 * c : P, g, cols],
+                        start=(c == 0),
+                        stop=(c == CHUNKS - 1),
+                    )
+                nc.scalar.activation(
+                    out=squares[:, nh, :],
+                    in_=tok_ps[nh][:],
+                    func=ACT.Square,
+                    accum_out=sumsq[:, nh : nh + 1],
+                )
+            total = e_pool.tile([P, 1], F32, name="total")
+            nc.gpsimd.tensor_tensor(out=total[:], in0=sumsq[:, 0:1], in1=sumsq[:, 1:2], op=ALU.add)
+            mean_eps = e_pool.tile([P, 1], F32, name="mean_eps")
+            nc.gpsimd.tensor_scalar(
+                out=mean_eps[:], in0=total[:], scalar1=1.0 / DOUT, scalar2=EPS,
+                op0=ALU.mult, op1=ALU.add,
+            )
+            rstd[0] = e_pool.tile([P, 1], F32, name="rstd")
+            nc.gpsimd.tensor_tensor(out=rstd[0][:], in0=mean_eps[:], in1=neg_half[:], op=ALU.pow)
+
+        def finish(g, j):
+            scaled = e_pool.tile([P, DOUT], F32, name="scaled")
+            for nh in range(N_HALVES):
+                cols = slice(nh * BANK, (nh + 1) * BANK)
+                nc.vector.scalar_tensor_tensor(
+                    out=scaled[:, cols],
+                    in0=tok_ps[nh][:],
+                    scalar=rstd[0][:, 0:1],
+                    in1=gain[:, cols],
+                    op0=ALU.mult,
+                    op1=ALU.mult,
+                )
+            result = e_pool.tile([P, DOUT], F32, name="result")
+            nc.vector.tensor_tensor(out=result[:], in0=scaled[:], in1=bias[:, g, :], op=ALU.add)
+            nc.sync.dma_start(out=out[j * P : (j + 1) * P, g, :], in_=result[:])
+
+        for k in range(CHUNKS):
+            load_chunk(k)
+        load_chunk(CHUNKS)
+        load_w2(0)
+        for k in range(CHUNKS + 1, RAW_BUFS):
+            load_chunk(k)
+        load_w2(1)
+
+        spread_row(ident_bf[:, 0:1], gain[:])
+        prepare_group(0)
+        for u in range(LOOK):
+            transpose_weights(u)
+
+        for u in range(N_UNITS + UNITS_PER_GROUP):
+            step = u % UNITS_PER_GROUP
+            g_done = u // UNITS_PER_GROUP - 1
+            live = u < N_UNITS
+            if live:
+                gate(u)
+            if g_done >= 0 and step == 2:
+                down_project(g_done, 0)
+            if g_done >= 0 and step == 5:
+                down_project(g_done, 1)
+                if g_done + W2_BUFS < GROUPS:
+                    load_w2(g_done + W2_BUFS)
+            if live:
+                value_and_product(u)
+            if u % UNITS_PER_CHUNK == 0 and 0 < u <= N_UNITS:
+                quantise(u // UNITS_PER_CHUNK - 1)
+            if g_done >= 0 and step == 3:
+                finish(g_done, 0)
+            if g_done >= 0 and step == 6:
+                finish(g_done, 1)
+            if step == 4 and g_done + 2 < GROUPS:
+                prepare_group(g_done + 2)
+            if u + LOOK < N_UNITS:
+                transpose_weights(u + LOOK)

@@ -32,11 +32,17 @@ B_TILES = BATCH // P
 BANK = 512
 N_HALVES = DOUT // BANK
 
-LOOK = 3
+LOOK = 2
+MX_LAG = 3
 RAW_BUFS = 8
-W2_BUFS = 2
+W2_BUFS = 8
 
 FLOPS = 2 * BATCH * GROUPS * (2 * RIN * HID + HID * DOUT)
+
+
+def pass_unit(k, j):
+    first_of_group = 1 if k % CHUNKS == 0 else 0
+    return UNITS_PER_CHUNK * k + j + MX_LAG + first_of_group
 
 
 def tile_observationembeddingv2_pb_e_kernel(
@@ -47,11 +53,12 @@ def tile_observationembeddingv2_pb_e_kernel(
         const = ctx.enter_context(tc.tile_pool(name="const", bufs=1))
         raw_pool = ctx.enter_context(tc.tile_pool(name="raw", bufs=RAW_BUFS))
         w2_pool = ctx.enter_context(tc.tile_pool(name="w2", bufs=W2_BUFS))
-        wt_pool = ctx.enter_context(tc.tile_pool(name="wt", bufs=LOOK + 1))
+        wt_pool = ctx.enter_context(tc.tile_pool(name="wt", bufs=LOOK + 2))
         h_pool = ctx.enter_context(tc.tile_pool(name="h", bufs=3))
-        q_pool = ctx.enter_context(tc.tile_pool(name="q", bufs=2))
-        e_pool = ctx.enter_context(tc.tile_pool(name="e", bufs=2))
-        psum = ctx.enter_context(tc.psum_pool(name="psum", bufs=2))
+        q_pool = ctx.enter_context(tc.tile_pool(name="q", bufs=4))
+        s_pool = ctx.enter_context(tc.tile_pool(name="s", bufs=2))
+        e_pool = ctx.enter_context(tc.tile_pool(name="e", bufs=4))
+        psum = ctx.enter_context(tc.psum_pool(name="psum", bufs=4))
         ctx.enter_context(tc.manual_schedule())
 
         ident = const.tile([P, P], F32, name="ident")
@@ -79,8 +86,8 @@ def tile_observationembeddingv2_pb_e_kernel(
             op=ALU.add,
         )
 
-        x_raw = const.tile([P, B_TILES, GROUPS * RIN], BF16, name="x_raw")
-        nc.sync.dma_start(out=x_raw[:], in_=xr.rearrange("(j p) g k -> p j (g k)", p=P))
+        x_raw = const.tile([P, B_TILES, GROUPS, RIN], BF16, name="x_raw")
+        x_dram = xr.rearrange("(j p) g k -> p j g k", p=P)
         x_words = x_raw[:].bitcast(F32)
         xT = const.tile([P, GROUPS, BATCH], F32, name="xT")
         xT_halves = xT[:].bitcast(BF16).rearrange("q g (b e) -> q g b e", e=2)
@@ -94,7 +101,7 @@ def tile_observationembeddingv2_pb_e_kernel(
         planes = {}
         grouped = {}
         silu_sb = {}
-        tok_ps = {}
+        tok = {}
         rstd = {}
 
         def load_chunk(k):
@@ -108,26 +115,26 @@ def tile_observationembeddingv2_pb_e_kernel(
                     ),
                 )
 
-        def load_w2(g):
-            for quad in range(4):
-                nc.sync.dma_start(
-                    out=w2_planes[32 * quad : 32 * quad + 16, g, :].bitcast(I32),
-                    in_=w2_r_scales[
-                        CHUNKS * g : CHUNKS * (g + 1), 4 * quad : 4 * quad + 4, :
-                    ].bitcast(I32),
-                )
-            w2_words[g] = w2_pool.tile([P, CHUNKS, DOUT], U32, name="w2_words", align_bytes=64)
+        def load_w2(k):
+            g, c = divmod(k, CHUNKS)
+            if c == 0:
+                for quad in range(4):
+                    nc.sync.dma_start(
+                        out=w2_planes[32 * quad : 32 * quad + 16, g, :].bitcast(I32),
+                        in_=w2_r_scales[
+                            CHUNKS * g : CHUNKS * (g + 1), 4 * quad : 4 * quad + 4, :
+                        ].bitcast(I32),
+                    )
+            w2_words[k] = w2_pool.tile([P, DOUT], U32, name="w2_words", align_bytes=64)
             nc.sync.dma_start(
-                out=w2_words[g][:].bitcast(I32),
-                in_=w2_r_words[CHUNKS * g : CHUNKS * (g + 1)]
-                .rearrange("c p n t -> p c (n t)")
-                .bitcast(I32),
+                out=w2_words[k][:].bitcast(I32),
+                in_=w2_r_words[k].rearrange("p n t -> p (n t)").bitcast(I32),
             )
 
-        def spread_row(pick, dest):
+        def spread_row(pick, dest, copy):
             for nh in range(N_HALVES):
                 cols = slice(nh * BANK, (nh + 1) * BANK)
-                spread_ps = psum.tile([P, BANK], F32, name="spread_ps", tag="av", bufs=4)
+                spread_ps = psum.tile([P, BANK], F32, name="spread_ps", tag="work")
                 nc.tensor.matmul(
                     out=spread_ps[:],
                     lhsT=pick.to_broadcast([P, P]),
@@ -135,21 +142,18 @@ def tile_observationembeddingv2_pb_e_kernel(
                     start=True,
                     stop=True,
                 )
-                nc.scalar.copy(out=dest[:, cols], in_=spread_ps[:])
+                copy(out=dest[:, cols], in_=spread_ps[:])
 
-        def prepare_group(g):
-            xt_ps = psum.tile([P, B_TILES, P], F32, name="xt_ps", tag="tr", bufs=2)
+        def transpose_x(g):
+            xt_ps = psum.tile([P, B_TILES, P], F32, name="xt_ps", tag="work")
             for j in range(B_TILES):
-                nc.tensor.transpose(
-                    xt_ps[:, j, :], x_words[:, j, g * P : (g + 1) * P], ident[:]
-                )
+                nc.tensor.transpose(xt_ps[:, j, :], x_words[:, j, g, :], ident[:])
             nc.scalar.copy(out=xT[:, g, :], in_=xt_ps[:].rearrange("q j b -> q (j b)"))
-            spread_row(pick_bias[:, g : g + 1], bias[:, g, :])
 
         def transpose_weights(u):
             k, half = divmod(u, UNITS_PER_CHUNK)
             raw_words = raw[k][:].bitcast(F32)
-            wt_ps = psum.tile([P, 2 * T_UNIT, P], F32, name="wt_ps", tag="tr", bufs=2)
+            wt_ps = psum.tile([P, 2 * T_UNIT, P], F32, name="wt_ps", tag="work")
             for i in range(2):
                 for tl in range(T_UNIT):
                     nc.tensor.transpose(
@@ -165,7 +169,7 @@ def tile_observationembeddingv2_pb_e_kernel(
         def project(u, i):
             g = u // UNITS_PER_GROUP
             halves = weights_t[u][:].bitcast(BF16).rearrange("q s (m e) -> q s m e", e=2)
-            acc = psum.tile([P, T_UNIT, BATCH], F32, name="acc", tag="av", bufs=4)
+            acc = psum.tile([P, T_UNIT, BATCH], F32, name="acc", tag="work")
             for tl in range(T_UNIT):
                 for e in range(2):
                     nc.tensor.matmul(
@@ -195,99 +199,109 @@ def tile_observationembeddingv2_pb_e_kernel(
             )
 
         def quantise(k):
-            g, c = divmod(k, CHUNKS)
-            if c == 0:
-                codes[g] = q_pool.tile([P, CHUNKS, BATCH], U32, name="codes", align_bytes=64)
-                planes[g] = q_pool.tile([P, CHUNKS, BATCH], U8, name="planes", align_bytes=64)
+            codes[k] = q_pool.tile([P, BATCH], U32, name="codes", align_bytes=64)
+            planes[k] = q_pool.tile([P, BATCH], U8, name="planes", align_bytes=64)
             nc.vector.quantize_mx(
-                out=codes[g][:, c, :].bitcast(FP8X4),
-                scales=planes[g][:, c, :],
+                out=codes[k][:].bitcast(FP8X4),
+                scales=planes[k][:],
                 in_=grouped[k][:].rearrange("p b t -> p (b t)"),
             )
 
-        def down_project(g, j):
+        def down_project(k, j):
+            g, c = divmod(k, CHUNKS)
             rows_b = slice(j * P, (j + 1) * P)
-            sumsq = e_pool.tile([P, N_HALVES], F32, name="sumsq")
-            squares = e_pool.tile([P, N_HALVES, BANK], BF16, name="squares")
             for nh in range(N_HALVES):
                 cols = slice(nh * BANK, (nh + 1) * BANK)
-                tok_ps[nh] = psum.tile([P, BANK], F32, name="tok_ps", tag="tok", bufs=2)
-                for c in range(CHUNKS):
-                    nc.tensor.matmul_mx(
-                        out=tok_ps[nh][:],
-                        lhsT=codes[g][:, c, rows_b].bitcast(FP8X4),
-                        lhsT_scale=planes[g][:, c, rows_b],
-                        rhs=w2_words[g][:, c, cols].bitcast(FP8X4),
-                        rhs_scale=w2_planes[4 * c : P, g, cols],
-                        start=(c == 0),
-                        stop=(c == CHUNKS - 1),
-                    )
+                if c == 0:
+                    tok[j, nh] = psum.tile([P, BANK], F32, name="tok", tag="tok")
+                nc.tensor.matmul_mx(
+                    out=tok[j, nh][:],
+                    lhsT=codes[k][:, rows_b].bitcast(FP8X4),
+                    lhsT_scale=planes[k][:, rows_b],
+                    rhs=w2_words[k][:, cols].bitcast(FP8X4),
+                    rhs_scale=w2_planes[4 * c : P, g, cols],
+                    start=(c == 0),
+                    stop=(c == CHUNKS - 1),
+                )
+            if j == B_TILES - 1 and k + W2_BUFS < N_CHUNKS:
+                load_w2(k + W2_BUFS)
+
+        def inverse_rms(j):
+            sumsq = s_pool.tile([P, N_HALVES], F32, name="sumsq")
+            squares = s_pool.tile([P, N_HALVES, BANK], BF16, name="squares")
+            for nh in range(N_HALVES):
                 nc.scalar.activation(
                     out=squares[:, nh, :],
-                    in_=tok_ps[nh][:],
+                    in_=tok[j, nh][:],
                     func=ACT.Square,
                     accum_out=sumsq[:, nh : nh + 1],
                 )
-            total = e_pool.tile([P, 1], F32, name="total")
+            total = s_pool.tile([P, 1], F32, name="total")
             nc.gpsimd.tensor_tensor(out=total[:], in0=sumsq[:, 0:1], in1=sumsq[:, 1:2], op=ALU.add)
-            mean_eps = e_pool.tile([P, 1], F32, name="mean_eps")
+            mean_eps = s_pool.tile([P, 1], F32, name="mean_eps")
             nc.gpsimd.tensor_scalar(
                 out=mean_eps[:], in0=total[:], scalar1=1.0 / DOUT, scalar2=EPS,
                 op0=ALU.mult, op1=ALU.add,
             )
-            rstd[0] = e_pool.tile([P, 1], F32, name="rstd")
-            nc.gpsimd.tensor_tensor(out=rstd[0][:], in0=mean_eps[:], in1=neg_half[:], op=ALU.pow)
+            rstd[j] = s_pool.tile([P, 1], F32, name="rstd")
+            nc.gpsimd.tensor_tensor(out=rstd[j][:], in0=mean_eps[:], in1=neg_half[:], op=ALU.pow)
 
         def finish(g, j):
-            scaled = e_pool.tile([P, DOUT], F32, name="scaled")
+            adder = nc.gpsimd if g < GROUPS - 1 else nc.vector
             for nh in range(N_HALVES):
                 cols = slice(nh * BANK, (nh + 1) * BANK)
+                scaled = e_pool.tile([P, BANK], F32, name="scaled")
                 nc.vector.scalar_tensor_tensor(
-                    out=scaled[:, cols],
-                    in0=tok_ps[nh][:],
-                    scalar=rstd[0][:, 0:1],
+                    out=scaled[:],
+                    in0=tok[j, nh][:],
+                    scalar=rstd[j][:, 0:1],
                     in1=gain[:, cols],
                     op0=ALU.mult,
                     op1=ALU.mult,
                 )
-            result = e_pool.tile([P, DOUT], F32, name="result")
-            nc.vector.tensor_tensor(out=result[:], in0=scaled[:], in1=bias[:, g, :], op=ALU.add)
-            nc.sync.dma_start(out=out[j * P : (j + 1) * P, g, :], in_=result[:])
+                result = e_pool.tile([P, BANK], F32, name="result")
+                adder.tensor_tensor(out=result[:], in0=scaled[:], in1=bias[:, g, cols], op=ALU.add)
+                nc.sync.dma_start(out=out[j * P : (j + 1) * P, g, cols], in_=result[:])
 
+        nc.sync.dma_start(out=x_raw[:, :, 0, :], in_=x_dram[:, :, 0, :])
         for k in range(CHUNKS):
             load_chunk(k)
-        load_chunk(CHUNKS)
-        load_w2(0)
-        for k in range(CHUNKS + 1, RAW_BUFS):
-            load_chunk(k)
-        load_w2(1)
+        nc.sync.dma_start(out=x_raw[:, :, 1:, :], in_=x_dram[:, :, 1:, :])
+        for k in range(W2_BUFS):
+            load_w2(k)
+            if k + CHUNKS < RAW_BUFS:
+                load_chunk(k + CHUNKS)
 
-        spread_row(ident_bf[:, 0:1], gain[:])
-        prepare_group(0)
-        for u in range(LOOK):
+        transpose_x(0)
+        transpose_weights(0)
+        spread_row(ident_bf[:, 0:1], gain[:], nc.vector.tensor_copy)
+        for u in range(1, LOOK):
             transpose_weights(u)
 
-        for u in range(N_UNITS + UNITS_PER_GROUP):
-            step = u % UNITS_PER_GROUP
-            g_done = u // UNITS_PER_GROUP - 1
+        last_chunk = [CHUNKS * g + CHUNKS - 1 for g in range(GROUPS)]
+        n_steps = pass_unit(N_CHUNKS - 1, B_TILES - 1) + 2
+        for u in range(n_steps):
+            g_now, step = divmod(u, UNITS_PER_GROUP)
             live = u < N_UNITS
             if live:
                 gate(u)
-            if g_done >= 0 and step == 2:
-                down_project(g_done, 0)
-            if g_done >= 0 and step == 5:
-                down_project(g_done, 1)
-                if g_done + W2_BUFS < GROUPS:
-                    load_w2(g_done + W2_BUFS)
-            if live:
-                value_and_product(u)
+            for k in range(N_CHUNKS):
+                for j in range(B_TILES):
+                    if pass_unit(k, j) == u:
+                        down_project(k, j)
+                        if k in last_chunk:
+                            inverse_rms(j)
             if u % UNITS_PER_CHUNK == 0 and 0 < u <= N_UNITS:
                 quantise(u // UNITS_PER_CHUNK - 1)
-            if g_done >= 0 and step == 3:
-                finish(g_done, 0)
-            if g_done >= 0 and step == 6:
-                finish(g_done, 1)
-            if step == 4 and g_done + 2 < GROUPS:
-                prepare_group(g_done + 2)
+            if live:
+                value_and_product(u)
+            for g in range(GROUPS):
+                for j in range(B_TILES):
+                    if pass_unit(last_chunk[g], j) + 1 == u:
+                        finish(g, j)
+            if live and step == 3:
+                spread_row(pick_bias[:, g_now : g_now + 1], bias[:, g_now, :], nc.scalar.copy)
+            if live and step == 5 and g_now + 1 < GROUPS:
+                transpose_x(g_now + 1)
             if u + LOOK < N_UNITS:
                 transpose_weights(u + LOOK)

@@ -24,25 +24,31 @@ EPS = 1e-05
 K_PASS = P * PACK
 CHUNKS = HID // K_PASS
 N_CHUNKS = GROUPS * CHUNKS
-UNITS_PER_CHUNK = 2
-UNITS_PER_GROUP = CHUNKS * UNITS_PER_CHUNK
-N_UNITS = GROUPS * UNITS_PER_GROUP
-T_UNIT = PACK // UNITS_PER_CHUNK
+HALVES = 2
+T_HALF = PACK // HALVES
 B_TILES = BATCH // P
 BANK = 512
 N_HALVES = DOUT // BANK
 
-LOOK = 2
-MX_LAG = 3
 RAW_BUFS = 8
 W2_BUFS = 8
 
 FLOPS = 2 * BATCH * GROUPS * (2 * RIN * HID + HID * DOUT)
 
 
-def pass_unit(k, j):
-    first_of_group = 1 if k % CHUNKS == 0 else 0
-    return UNITS_PER_CHUNK * k + j + MX_LAG + first_of_group
+def mx_plan():
+    plan = {}
+    for g in range(GROUPS):
+        for c in range(CHUNKS):
+            for j in range(B_TILES):
+                for nh in range(N_HALVES):
+                    if g < GROUPS - 1:
+                        if c == 0:
+                            plan.setdefault(CHUNKS * (g + 1) + j, []).append((g, j, nh, list(range(CHUNKS))))
+                    else:
+                        step = max(CHUNKS * g + c + 1, CHUNKS * g + 2)
+                        plan.setdefault(step, []).append((g, j, nh, [c]))
+    return plan
 
 
 def tile_observationembeddingv2_pb_e_kernel(
@@ -53,12 +59,12 @@ def tile_observationembeddingv2_pb_e_kernel(
         const = ctx.enter_context(tc.tile_pool(name="const", bufs=1))
         raw_pool = ctx.enter_context(tc.tile_pool(name="raw", bufs=RAW_BUFS))
         w2_pool = ctx.enter_context(tc.tile_pool(name="w2", bufs=W2_BUFS))
-        wt_pool = ctx.enter_context(tc.tile_pool(name="wt", bufs=LOOK + 2))
-        h_pool = ctx.enter_context(tc.tile_pool(name="h", bufs=3))
-        q_pool = ctx.enter_context(tc.tile_pool(name="q", bufs=4))
-        s_pool = ctx.enter_context(tc.tile_pool(name="s", bufs=2))
+        wt_pool = ctx.enter_context(tc.tile_pool(name="wt", bufs=3))
+        h_pool = ctx.enter_context(tc.tile_pool(name="h", bufs=4))
+        q_pool = ctx.enter_context(tc.tile_pool(name="q", bufs=8))
+        s_pool = ctx.enter_context(tc.tile_pool(name="s", bufs=4))
         e_pool = ctx.enter_context(tc.tile_pool(name="e", bufs=4))
-        psum = ctx.enter_context(tc.psum_pool(name="psum", bufs=4))
+        psum = ctx.enter_context(tc.psum_pool(name="psum", bufs=8))
         ctx.enter_context(tc.manual_schedule())
 
         ident = const.tile([P, P], F32, name="ident")
@@ -102,7 +108,9 @@ def tile_observationembeddingv2_pb_e_kernel(
         grouped = {}
         silu_sb = {}
         tok = {}
+        sumsq = {}
         rstd = {}
+        scaled = {}
 
         def load_chunk(k):
             g, c = divmod(k, CHUNKS)
@@ -134,7 +142,7 @@ def tile_observationembeddingv2_pb_e_kernel(
         def spread_row(pick, dest, copy):
             for nh in range(N_HALVES):
                 cols = slice(nh * BANK, (nh + 1) * BANK)
-                spread_ps = psum.tile([P, BANK], F32, name="spread_ps", tag="work")
+                spread_ps = psum.tile([P, BANK], F32, name="spread_ps", tag="bank")
                 nc.tensor.matmul(
                     out=spread_ps[:],
                     lhsT=pick.to_broadcast([P, P]),
@@ -145,56 +153,50 @@ def tile_observationembeddingv2_pb_e_kernel(
                 copy(out=dest[:, cols], in_=spread_ps[:])
 
         def transpose_x(g):
-            xt_ps = psum.tile([P, B_TILES, P], F32, name="xt_ps", tag="work")
+            xt_ps = psum.tile([P, B_TILES, P], F32, name="xt_ps", tag="bank")
             for j in range(B_TILES):
                 nc.tensor.transpose(xt_ps[:, j, :], x_words[:, j, g, :], ident[:])
             nc.scalar.copy(out=xT[:, g, :], in_=xt_ps[:].rearrange("q j b -> q (j b)"))
 
-        def transpose_weights(u):
-            k, half = divmod(u, UNITS_PER_CHUNK)
+        def transpose_weights(k):
             raw_words = raw[k][:].bitcast(F32)
-            wt_ps = psum.tile([P, 2 * T_UNIT, P], F32, name="wt_ps", tag="work")
+            weights_t[k] = wt_pool.tile([P, 2, PACK, P], F32, name="weights_t")
             for i in range(2):
-                for tl in range(T_UNIT):
-                    nc.tensor.transpose(
-                        wt_ps[:, i * T_UNIT + tl, :],
-                        raw_words[:, i, half * T_UNIT + tl, :],
-                        ident[:],
-                    )
-            weights_t[u] = wt_pool.tile([P, 2 * T_UNIT, P], F32, name="weights_t")
-            nc.scalar.copy(out=weights_t[u][:], in_=wt_ps[:])
-            if half == UNITS_PER_CHUNK - 1 and k + RAW_BUFS < N_CHUNKS:
+                wt_ps = psum.tile([P, PACK, P], F32, name="wt_ps", tag="bank")
+                for t in range(PACK):
+                    nc.tensor.transpose(wt_ps[:, t, :], raw_words[:, i, t, :], ident[:])
+                nc.scalar.copy(out=weights_t[k][:, i], in_=wt_ps[:])
+            if k + RAW_BUFS < N_CHUNKS:
                 load_chunk(k + RAW_BUFS)
 
-        def project(u, i):
-            g = u // UNITS_PER_GROUP
-            halves = weights_t[u][:].bitcast(BF16).rearrange("q s (m e) -> q s m e", e=2)
-            acc = psum.tile([P, T_UNIT, BATCH], F32, name="acc", tag="work")
-            for tl in range(T_UNIT):
+        def project(k, half, i):
+            g = k // CHUNKS
+            pairs = weights_t[k][:].bitcast(BF16).rearrange("q i t (m e) -> q i t m e", e=2)
+            acc = psum.tile([P, T_HALF, BATCH], F32, name="acc", tag="bank")
+            for tl in range(T_HALF):
                 for e in range(2):
                     nc.tensor.matmul(
                         out=acc[:, tl, :],
-                        lhsT=halves[:, i * T_UNIT + tl, :, e],
+                        lhsT=pairs[:, i, half * T_HALF + tl, :, e],
                         rhs=xT_halves[:, g, :, e],
                         start=(e == 0),
                         stop=(e == 1),
                     )
             return acc
 
-        def gate(u):
-            gate_ps = project(u, 0)
-            silu_sb[u] = h_pool.tile([P, T_UNIT, BATCH], F32, name="silu_sb")
-            nc.scalar.activation(out=silu_sb[u][:], in_=gate_ps[:], func=ACT.Silu)
+        def gate(k, half):
+            gate_ps = project(k, half, 0)
+            silu_sb[k, half] = h_pool.tile([P, T_HALF, BATCH], F32, name="silu_sb")
+            nc.scalar.activation(out=silu_sb[k, half][:], in_=gate_ps[:], func=ACT.Silu)
 
-        def value_and_product(u):
-            k, half = divmod(u, UNITS_PER_CHUNK)
-            value_ps = project(u, 1)
+        def value_and_product(k, half):
+            value_ps = project(k, half, 1)
             if half == 0:
                 grouped[k] = h_pool.tile([P, BATCH, PACK], BF16, name="grouped", align_bytes=64)
             nc.vector.tensor_tensor(
-                out=grouped[k][:, :, half * T_UNIT : (half + 1) * T_UNIT],
+                out=grouped[k][:, :, half * T_HALF : (half + 1) * T_HALF],
                 in0=value_ps[:].rearrange("p t b -> p b t"),
-                in1=silu_sb[u][:].rearrange("p t b -> p b t"),
+                in1=silu_sb[k, half][:].rearrange("p t b -> p b t"),
                 op=ALU.mult,
             )
 
@@ -207,13 +209,13 @@ def tile_observationembeddingv2_pb_e_kernel(
                 in_=grouped[k][:].rearrange("p b t -> p (b t)"),
             )
 
-        def down_project(k, j):
-            g, c = divmod(k, CHUNKS)
+        def down_project(g, j, nh, chunks):
             rows_b = slice(j * P, (j + 1) * P)
-            for nh in range(N_HALVES):
-                cols = slice(nh * BANK, (nh + 1) * BANK)
+            cols = slice(nh * BANK, (nh + 1) * BANK)
+            for c in chunks:
+                k = CHUNKS * g + c
                 if c == 0:
-                    tok[j, nh] = psum.tile([P, BANK], F32, name="tok", tag="tok")
+                    tok[j, nh] = psum.tile([P, BANK], F32, name="tok", tag="bank")
                 nc.tensor.matmul_mx(
                     out=tok[j, nh][:],
                     lhsT=codes[k][:, rows_b].bitcast(FP8X4),
@@ -223,21 +225,23 @@ def tile_observationembeddingv2_pb_e_kernel(
                     start=(c == 0),
                     stop=(c == CHUNKS - 1),
                 )
-            if j == B_TILES - 1 and k + W2_BUFS < N_CHUNKS:
-                load_w2(k + W2_BUFS)
+                if j == B_TILES - 1 and nh == N_HALVES - 1 and k + W2_BUFS < N_CHUNKS:
+                    load_w2(k + W2_BUFS)
+
+        def sum_squares(j, nh):
+            if nh == 0:
+                sumsq[j] = s_pool.tile([P, N_HALVES], F32, name="sumsq")
+            squares = s_pool.tile([P, BANK], BF16, name="squares")
+            nc.scalar.activation(
+                out=squares[:],
+                in_=tok[j, nh][:],
+                func=ACT.Square,
+                accum_out=sumsq[j][:, nh : nh + 1],
+            )
 
         def inverse_rms(j):
-            sumsq = s_pool.tile([P, N_HALVES], F32, name="sumsq")
-            squares = s_pool.tile([P, N_HALVES, BANK], BF16, name="squares")
-            for nh in range(N_HALVES):
-                nc.scalar.activation(
-                    out=squares[:, nh, :],
-                    in_=tok[j, nh][:],
-                    func=ACT.Square,
-                    accum_out=sumsq[:, nh : nh + 1],
-                )
             total = s_pool.tile([P, 1], F32, name="total")
-            nc.gpsimd.tensor_tensor(out=total[:], in0=sumsq[:, 0:1], in1=sumsq[:, 1:2], op=ALU.add)
+            nc.gpsimd.tensor_tensor(out=total[:], in0=sumsq[j][:, 0:1], in1=sumsq[j][:, 1:2], op=ALU.add)
             mean_eps = s_pool.tile([P, 1], F32, name="mean_eps")
             nc.gpsimd.tensor_scalar(
                 out=mean_eps[:], in0=total[:], scalar1=1.0 / DOUT, scalar2=EPS,
@@ -246,22 +250,23 @@ def tile_observationembeddingv2_pb_e_kernel(
             rstd[j] = s_pool.tile([P, 1], F32, name="rstd")
             nc.gpsimd.tensor_tensor(out=rstd[j][:], in0=mean_eps[:], in1=neg_half[:], op=ALU.pow)
 
-        def finish(g, j):
-            adder = nc.gpsimd if g < GROUPS - 1 else nc.vector
-            for nh in range(N_HALVES):
-                cols = slice(nh * BANK, (nh + 1) * BANK)
-                scaled = e_pool.tile([P, BANK], F32, name="scaled")
-                nc.vector.scalar_tensor_tensor(
-                    out=scaled[:],
-                    in0=tok[j, nh][:],
-                    scalar=rstd[j][:, 0:1],
-                    in1=gain[:, cols],
-                    op0=ALU.mult,
-                    op1=ALU.mult,
-                )
-                result = e_pool.tile([P, BANK], F32, name="result")
-                adder.tensor_tensor(out=result[:], in0=scaled[:], in1=bias[:, g, cols], op=ALU.add)
-                nc.sync.dma_start(out=out[j * P : (j + 1) * P, g, cols], in_=result[:])
+        def scale_tok(j, nh):
+            cols = slice(nh * BANK, (nh + 1) * BANK)
+            scaled[j, nh] = e_pool.tile([P, BANK], F32, name="scaled")
+            nc.vector.scalar_tensor_tensor(
+                out=scaled[j, nh][:],
+                in0=tok[j, nh][:],
+                scalar=rstd[j][:, 0:1],
+                in1=gain[:, cols],
+                op0=ALU.mult,
+                op1=ALU.mult,
+            )
+
+        def add_bias_and_store(g, j, nh):
+            cols = slice(nh * BANK, (nh + 1) * BANK)
+            result = e_pool.tile([P, BANK], F32, name="result")
+            nc.vector.tensor_tensor(out=result[:], in0=scaled[j, nh][:], in1=bias[:, g, cols], op=ALU.add)
+            nc.sync.dma_start(out=out[j * P : (j + 1) * P, g, cols], in_=result[:])
 
         nc.sync.dma_start(out=x_raw[:, :, 0, :], in_=x_dram[:, :, 0, :])
         for k in range(CHUNKS):
@@ -275,33 +280,37 @@ def tile_observationembeddingv2_pb_e_kernel(
         transpose_x(0)
         transpose_weights(0)
         spread_row(ident_bf[:, 0:1], gain[:], nc.vector.tensor_copy)
-        for u in range(1, LOOK):
-            transpose_weights(u)
 
-        last_chunk = [CHUNKS * g + CHUNKS - 1 for g in range(GROUPS)]
-        n_steps = pass_unit(N_CHUNKS - 1, B_TILES - 1) + 2
-        for u in range(n_steps):
-            g_now, step = divmod(u, UNITS_PER_GROUP)
-            live = u < N_UNITS
+        plan = mx_plan()
+        closed = []
+        for s in range(max(plan) + 2):
+            g_now, c_now = divmod(s, CHUNKS)
+            live = s < N_CHUNKS
             if live:
-                gate(u)
-            for k in range(N_CHUNKS):
-                for j in range(B_TILES):
-                    if pass_unit(k, j) == u:
-                        down_project(k, j)
-                        if k in last_chunk:
-                            inverse_rms(j)
-            if u % UNITS_PER_CHUNK == 0 and 0 < u <= N_UNITS:
-                quantise(u // UNITS_PER_CHUNK - 1)
+                gate(s, 0)
+                gate(s, 1)
+            if 0 < s <= N_CHUNKS:
+                quantise(s - 1)
+            if s + 1 < N_CHUNKS:
+                transpose_weights(s + 1)
+            for g, j in closed:
+                for nh in range(N_HALVES):
+                    scale_tok(j, nh)
             if live:
-                value_and_product(u)
-            for g in range(GROUPS):
-                for j in range(B_TILES):
-                    if pass_unit(last_chunk[g], j) + 1 == u:
-                        finish(g, j)
-            if live and step == 3:
+                value_and_product(s, 0)
+                value_and_product(s, 1)
+            for g, j in closed:
+                for nh in range(N_HALVES):
+                    add_bias_and_store(g, j, nh)
+            closed = []
+            for g, j, nh, chunks in plan.get(s, []):
+                down_project(g, j, nh, chunks)
+                if CHUNKS - 1 in chunks:
+                    sum_squares(j, nh)
+                    if nh == N_HALVES - 1:
+                        inverse_rms(j)
+                        closed.append((g, j))
+            if live and c_now == 1:
                 spread_row(pick_bias[:, g_now : g_now + 1], bias[:, g_now, :], nc.scalar.copy)
-            if live and step == 5 and g_now + 1 < GROUPS:
+            if live and c_now == 2 and g_now + 1 < GROUPS:
                 transpose_x(g_now + 1)
-            if u + LOOK < N_UNITS:
-                transpose_weights(u + LOOK)

@@ -67,20 +67,17 @@ def tile_observationembeddingv2_pb_e_kernel(
         psum = ctx.enter_context(tc.psum_pool(name="psum", bufs=8))
         ctx.enter_context(tc.manual_schedule())
 
-        ident = const.tile([P, P], F32, name="ident")
-        make_identity(nc, ident[:])
         neg_half = const.tile([P, 1], F32, name="neg_half")
         nc.gpsimd.memset(neg_half[:], -0.5)
+        warm = const.tile([P, 1], F32, name="warm")
+        nc.scalar.activation(out=warm[:], in_=neg_half[:], func=ACT.Silu)
+        ident = const.tile([P, P], F32, name="ident")
+        make_identity(nc, ident[:])
 
         rows = const.tile([P, DOUT], BF16, name="rows")
         nc.vector.memset(rows[:], 0.0)
         w2_planes = const.tile([P, GROUPS, DOUT], U8, name="w2_planes", align_bytes=64)
         nc.vector.memset(w2_planes[:].bitcast(I32), 0)
-        nc.scalar.dma_start(out=rows[0:1, :], in_=norm_w.unsqueeze(0))
-        nc.scalar.dma_start(out=rows[1:2, :], in_=norm_b.unsqueeze(0))
-        nc.scalar.dma_start(out=rows[2 : 2 + GROUPS, :], in_=term_embed_r)
-        warm = const.tile([P, 1], F32, name="warm")
-        nc.scalar.activation(out=warm[:], in_=neg_half[:], func=ACT.Silu)
 
         ident_bf = const.tile([P, P], BF16, name="ident_bf")
         nc.vector.tensor_copy(out=ident_bf[:], in_=ident[:])
@@ -92,9 +89,9 @@ def tile_observationembeddingv2_pb_e_kernel(
             op=ALU.add,
         )
 
-        x_raw = const.tile([P, B_TILES, GROUPS, RIN], BF16, name="x_raw")
+        x_first = const.tile([P, B_TILES, 1, RIN], BF16, name="x_first")
+        x_rest = const.tile([P, B_TILES, GROUPS - 1, RIN], BF16, name="x_rest")
         x_dram = xr.rearrange("(j p) g k -> p j g k", p=P)
-        x_words = x_raw[:].bitcast(F32)
         xT = const.tile([P, GROUPS, BATCH], F32, name="xT")
         xT_halves = xT[:].bitcast(BF16).rearrange("q g (b e) -> q g b e", e=2)
         gain = const.tile([P, DOUT], F32, name="gain")
@@ -154,8 +151,9 @@ def tile_observationembeddingv2_pb_e_kernel(
 
         def transpose_x(g):
             xt_ps = psum.tile([P, B_TILES, P], F32, name="xt_ps", tag="bank")
+            x_words = (x_first if g == 0 else x_rest)[:].bitcast(F32)
             for j in range(B_TILES):
-                nc.tensor.transpose(xt_ps[:, j, :], x_words[:, j, g, :], ident[:])
+                nc.tensor.transpose(xt_ps[:, j, :], x_words[:, j, max(g - 1, 0), :], ident[:])
             nc.scalar.copy(out=xT[:, g, :], in_=xt_ps[:].rearrange("q j b -> q (j b)"))
 
         def transpose_weights(k):
@@ -236,16 +234,15 @@ def tile_observationembeddingv2_pb_e_kernel(
                 out=squares[:],
                 in_=tok[j, nh][:],
                 func=ACT.Square,
+                scale=DOUT ** -0.5,
                 accum_out=sumsq[j][:, nh : nh + 1],
             )
 
         def inverse_rms(j):
-            total = s_pool.tile([P, 1], F32, name="total")
-            nc.gpsimd.tensor_tensor(out=total[:], in0=sumsq[j][:, 0:1], in1=sumsq[j][:, 1:2], op=ALU.add)
             mean_eps = s_pool.tile([P, 1], F32, name="mean_eps")
             nc.gpsimd.tensor_scalar(
-                out=mean_eps[:], in0=total[:], scalar1=1.0 / DOUT, scalar2=EPS,
-                op0=ALU.mult, op1=ALU.add,
+                out=mean_eps[:], in0=sumsq[j][:, 0:1], scalar1=sumsq[j][:, 1:2], scalar2=EPS,
+                op0=ALU.add, op1=ALU.add,
             )
             rstd[j] = s_pool.tile([P, 1], F32, name="rstd")
             nc.gpsimd.tensor_tensor(out=rstd[j][:], in0=mean_eps[:], in1=neg_half[:], op=ALU.pow)
@@ -265,13 +262,17 @@ def tile_observationembeddingv2_pb_e_kernel(
         def add_bias_and_store(g, j, nh):
             cols = slice(nh * BANK, (nh + 1) * BANK)
             result = e_pool.tile([P, BANK], F32, name="result")
-            nc.vector.tensor_tensor(out=result[:], in0=scaled[j, nh][:], in1=bias[:, g, cols], op=ALU.add)
+            adder = nc.gpsimd if g == GROUPS - 1 and j == 0 else nc.vector
+            adder.tensor_tensor(out=result[:], in0=scaled[j, nh][:], in1=bias[:, g, cols], op=ALU.add)
             nc.sync.dma_start(out=out[j * P : (j + 1) * P, g, cols], in_=result[:])
 
-        nc.sync.dma_start(out=x_raw[:, :, 0, :], in_=x_dram[:, :, 0, :])
+        nc.sync.dma_start(out=x_first[:], in_=x_dram[:, :, 0:1, :])
         for k in range(CHUNKS):
             load_chunk(k)
-        nc.sync.dma_start(out=x_raw[:, :, 1:, :], in_=x_dram[:, :, 1:, :])
+        nc.sync.dma_start(out=rows[0:1, :], in_=norm_w.unsqueeze(0))
+        nc.sync.dma_start(out=rows[1:2, :], in_=norm_b.unsqueeze(0))
+        nc.sync.dma_start(out=rows[2 : 2 + GROUPS, :], in_=term_embed_r)
+        nc.sync.dma_start(out=x_rest[:], in_=x_dram[:, :, 1:, :])
         for k in range(W2_BUFS):
             load_w2(k)
             if k + CHUNKS < RAW_BUFS:
@@ -279,7 +280,6 @@ def tile_observationembeddingv2_pb_e_kernel(
 
         transpose_x(0)
         transpose_weights(0)
-        spread_row(ident_bf[:, 0:1], gain[:], nc.vector.tensor_copy)
 
         plan = mx_plan()
         closed = []
@@ -310,6 +310,8 @@ def tile_observationembeddingv2_pb_e_kernel(
                     if nh == N_HALVES - 1:
                         inverse_rms(j)
                         closed.append((g, j))
+            if s == 0:
+                spread_row(ident_bf[:, 0:1], gain[:], nc.scalar.copy)
             if live and c_now == 1:
                 spread_row(pick_bias[:, g_now : g_now + 1], bias[:, g_now, :], nc.scalar.copy)
             if live and c_now == 2 and g_now + 1 < GROUPS:

@@ -92,8 +92,7 @@ def tile_observationembeddingv2_pb_e_kernel(
         x_first = const.tile([P, B_TILES, 1, RIN], BF16, name="x_first")
         x_rest = const.tile([P, B_TILES, GROUPS - 1, RIN], BF16, name="x_rest")
         x_dram = xr.rearrange("(j p) g k -> p j g k", p=P)
-        xT = const.tile([P, GROUPS, BATCH], F32, name="xT")
-        xT_halves = xT[:].bitcast(BF16).rearrange("q g (b e) -> q g b e", e=2)
+        xT = const.tile([P, GROUPS, 2, BATCH], BF16, name="xT")
         gain = const.tile([P, DOUT], F32, name="gain")
         bias = const.tile([P, GROUPS, DOUT], F32, name="bias")
 
@@ -154,7 +153,10 @@ def tile_observationembeddingv2_pb_e_kernel(
             x_words = (x_first if g == 0 else x_rest)[:].bitcast(F32)
             for j in range(B_TILES):
                 nc.tensor.transpose(xt_ps[:, j, :], x_words[:, j, max(g - 1, 0), :], ident[:])
-            nc.scalar.copy(out=xT[:, g, :], in_=xt_ps[:].rearrange("q j b -> q (j b)"))
+            nc.scalar.copy(
+                out=xT[:, g],
+                in_=xt_ps[:].rearrange("q j b -> q (j b)").bitcast(BF16).rearrange("q (b e) -> q e b", e=2),
+            )
 
         def transpose_weights(k):
             raw_words = raw[k][:].bitcast(F32)
@@ -176,7 +178,7 @@ def tile_observationembeddingv2_pb_e_kernel(
                     nc.tensor.matmul(
                         out=acc[:, tl, :],
                         lhsT=pairs[:, i, half * T_HALF + tl, :, e],
-                        rhs=xT_halves[:, g, :, e],
+                        rhs=xT[:, g, e, :],
                         start=(e == 0),
                         stop=(e == 1),
                     )

@@ -46,7 +46,8 @@ def mx_plan():
                         if c == 0:
                             plan.setdefault(CHUNKS * (g + 1) + j, []).append((g, j, nh, list(range(CHUNKS))))
                     else:
-                        step = max(CHUNKS * g + c + 1, CHUNKS * g + 2)
+                        k = CHUNKS * g + c
+                        step = max(k + 1, min(k + 2, N_CHUNKS - 1))
                         plan.setdefault(step, []).append((g, j, nh, [c]))
     return plan
 
@@ -249,23 +250,22 @@ def tile_observationembeddingv2_pb_e_kernel(
             rstd[j] = s_pool.tile([P, 1], F32, name="rstd")
             nc.gpsimd.tensor_tensor(out=rstd[j][:], in0=mean_eps[:], in1=neg_half[:], op=ALU.pow)
 
-        def scale_tok(j, nh):
+        def apply_gain(j, nh):
             cols = slice(nh * BANK, (nh + 1) * BANK)
             scaled[j, nh] = e_pool.tile([P, BANK], F32, name="scaled")
-            nc.vector.scalar_tensor_tensor(
-                out=scaled[j, nh][:],
-                in0=tok[j, nh][:],
-                scalar=rstd[j][:, 0:1],
-                in1=gain[:, cols],
-                op0=ALU.mult,
-                op1=ALU.mult,
-            )
+            nc.vector.tensor_tensor(out=scaled[j, nh][:], in0=tok[j, nh][:], in1=gain[:, cols], op=ALU.mult)
 
-        def add_bias_and_store(g, j, nh):
+        def normalise_and_store(g, j, nh):
             cols = slice(nh * BANK, (nh + 1) * BANK)
             result = e_pool.tile([P, BANK], F32, name="result")
-            adder = nc.gpsimd if g == GROUPS - 1 and j == 0 else nc.vector
-            adder.tensor_tensor(out=result[:], in0=scaled[j, nh][:], in1=bias[:, g, cols], op=ALU.add)
+            nc.vector.scalar_tensor_tensor(
+                out=result[:],
+                in0=scaled[j, nh][:],
+                scalar=rstd[j][:, 0:1],
+                in1=bias[:, g, cols],
+                op0=ALU.mult,
+                op1=ALU.add,
+            )
             nc.sync.dma_start(out=out[j * P : (j + 1) * P, g, cols], in_=result[:])
 
         nc.sync.dma_start(out=x_first[:], in_=x_dram[:, :, 0:1, :])
@@ -297,18 +297,16 @@ def tile_observationembeddingv2_pb_e_kernel(
                 transpose_weights(s + 1)
             for g, j in closed:
                 for nh in range(N_HALVES):
-                    scale_tok(j, nh)
+                    normalise_and_store(g, j, nh)
             if live:
                 value_and_product(s, 0)
                 value_and_product(s, 1)
-            for g, j in closed:
-                for nh in range(N_HALVES):
-                    add_bias_and_store(g, j, nh)
             closed = []
             for g, j, nh, chunks in plan.get(s, []):
                 down_project(g, j, nh, chunks)
                 if CHUNKS - 1 in chunks:
                     sum_squares(j, nh)
+                    apply_gain(j, nh)
                     if nh == N_HALVES - 1:
                         inverse_rms(j)
                         closed.append((g, j))

@@ -30,6 +30,7 @@ B_TILES = BATCH // P
 BANK = 512
 N_HALVES = DOUT // BANK
 
+T_STEPS = 2
 RAW_BUFS = 8
 W2_BUFS = 8
 
@@ -60,7 +61,7 @@ def tile_observationembeddingv2_pb_e_kernel(
         const = ctx.enter_context(tc.tile_pool(name="const", bufs=1))
         raw_pool = ctx.enter_context(tc.tile_pool(name="raw", bufs=RAW_BUFS))
         w2_pool = ctx.enter_context(tc.tile_pool(name="w2", bufs=W2_BUFS))
-        wt_pool = ctx.enter_context(tc.tile_pool(name="wt", bufs=3))
+        wt_pool = ctx.enter_context(tc.tile_pool(name="wt", bufs=T_STEPS + 2))
         h_pool = ctx.enter_context(tc.tile_pool(name="h", bufs=4))
         q_pool = ctx.enter_context(tc.tile_pool(name="q", bufs=8))
         s_pool = ctx.enter_context(tc.tile_pool(name="s", bufs=4))
@@ -293,8 +294,9 @@ def tile_observationembeddingv2_pb_e_kernel(
                 gate(s, 1)
             if 0 < s <= N_CHUNKS:
                 quantise(s - 1)
-            if s + 1 < N_CHUNKS:
-                transpose_weights(s + 1)
+            if s % T_STEPS == 0:
+                for k in range(s + 1, min(s + 1 + T_STEPS, N_CHUNKS)):
+                    transpose_weights(k)
             for g, j in closed:
                 for nh in range(N_HALVES):
                     normalise_and_store(g, j, nh)

@@ -30,7 +30,8 @@ B_TILES = BATCH // P
 BANK = 512
 N_HALVES = DOUT // BANK
 
-T_STEPS = 2
+AHEAD = 2
+M_STEP = 16
 RAW_BUFS = 8
 W2_BUFS = 8
 
@@ -61,7 +62,7 @@ def tile_observationembeddingv2_pb_e_kernel(
         const = ctx.enter_context(tc.tile_pool(name="const", bufs=1))
         raw_pool = ctx.enter_context(tc.tile_pool(name="raw", bufs=RAW_BUFS))
         w2_pool = ctx.enter_context(tc.tile_pool(name="w2", bufs=W2_BUFS))
-        wt_pool = ctx.enter_context(tc.tile_pool(name="wt", bufs=T_STEPS + 2))
+        wt_pool = ctx.enter_context(tc.tile_pool(name="wt", bufs=AHEAD + 2))
         h_pool = ctx.enter_context(tc.tile_pool(name="h", bufs=4))
         q_pool = ctx.enter_context(tc.tile_pool(name="q", bufs=8))
         s_pool = ctx.enter_context(tc.tile_pool(name="s", bufs=4))
@@ -101,6 +102,7 @@ def tile_observationembeddingv2_pb_e_kernel(
         raw = {}
         w2_words = {}
         weights_t = {}
+        wt_ps = {}
         codes = {}
         planes = {}
         grouped = {}
@@ -160,18 +162,21 @@ def tile_observationembeddingv2_pb_e_kernel(
                 in_=xt_ps[:].rearrange("q j b -> q (j b)").bitcast(BF16).rearrange("q (b e) -> q e b", e=2),
             )
 
-        def transpose_weights(k):
-            raw_words = raw[k][:].bitcast(F32)
-            weights_t[k] = wt_pool.tile([P, 2, PACK, P], F32, name="weights_t")
-            for i in range(2):
-                wt_ps = psum.tile([P, PACK, P], F32, name="wt_ps", tag="bank")
-                for t in range(PACK):
-                    nc.tensor.transpose(wt_ps[:, t, :], raw_words[:, i, t, :], ident[:])
-                nc.scalar.copy(out=weights_t[k][:, i], in_=wt_ps[:])
-            if k + RAW_BUFS < N_CHUNKS:
-                load_chunk(k + RAW_BUFS)
+        def transpose_one(k, i, t):
+            if i == 0 and t == 0:
+                weights_t[k] = wt_pool.tile([P, 2, PACK, P], F32, name="weights_t")
+            if t == 0:
+                wt_ps[k, i] = psum.tile([P, PACK, P], F32, name="wt_ps", tag="bank")
+            nc.tensor.transpose(wt_ps[k, i][:, t, :], raw[k][:].bitcast(F32)[:, i, t, :], ident[:])
+            if t == PACK - 1:
+                nc.scalar.copy(out=weights_t[k][:, i], in_=wt_ps[k, i][:])
+                if i == 1 and k + RAW_BUFS < N_CHUNKS:
+                    load_chunk(k + RAW_BUFS)
 
-        def project(k, half, i):
+        def chunk_transposes(k):
+            return [(k, i, t) for i in range(2) for t in range(PACK)]
+
+        def project(k, half, i, woven):
             g = k // CHUNKS
             pairs = weights_t[k][:].bitcast(BF16).rearrange("q i t (m e) -> q i t m e", e=2)
             acc = psum.tile([P, T_HALF, BATCH], F32, name="acc", tag="bank")
@@ -184,15 +189,20 @@ def tile_observationembeddingv2_pb_e_kernel(
                         start=(e == 0),
                         stop=(e == 1),
                     )
+                    m = ((i * HALVES + half) * T_HALF + tl) * 2 + e
+                    first = (m * len(woven) + M_STEP - 1) // M_STEP
+                    behind = ((m + 1) * len(woven) + M_STEP - 1) // M_STEP
+                    for task in woven[first:behind]:
+                        transpose_one(*task)
             return acc
 
-        def gate(k, half):
-            gate_ps = project(k, half, 0)
+        def gate(k, half, woven):
+            gate_ps = project(k, half, 0, woven)
             silu_sb[k, half] = h_pool.tile([P, T_HALF, BATCH], F32, name="silu_sb")
             nc.scalar.activation(out=silu_sb[k, half][:], in_=gate_ps[:], func=ACT.Silu)
 
-        def value_and_product(k, half):
-            value_ps = project(k, half, 1)
+        def value_and_product(k, half, woven):
+            value_ps = project(k, half, 1, woven)
             if half == 0:
                 grouped[k] = h_pool.tile([P, BATCH, PACK], BF16, name="grouped", align_bytes=64)
             nc.vector.tensor_tensor(
@@ -282,27 +292,28 @@ def tile_observationembeddingv2_pb_e_kernel(
                 load_chunk(k + CHUNKS)
 
         transpose_x(0)
-        transpose_weights(0)
+        for task in chunk_transposes(0):
+            transpose_one(*task)
 
         plan = mx_plan()
         closed = []
         for s in range(max(plan) + 2):
             g_now, c_now = divmod(s, CHUNKS)
             live = s < N_CHUNKS
+            woven = []
+            for k in range(1 if s == 0 else s + AHEAD, min(s + AHEAD + 1, N_CHUNKS)):
+                woven.extend(chunk_transposes(k))
             if live:
-                gate(s, 0)
-                gate(s, 1)
+                gate(s, 0, woven)
+                gate(s, 1, woven)
             if 0 < s <= N_CHUNKS:
                 quantise(s - 1)
-            if s % T_STEPS == 0:
-                for k in range(s + 1, min(s + 1 + T_STEPS, N_CHUNKS)):
-                    transpose_weights(k)
             for g, j in closed:
                 for nh in range(N_HALVES):
                     normalise_and_store(g, j, nh)
             if live:
-                value_and_product(s, 0)
-                value_and_product(s, 1)
+                value_and_product(s, 0, woven)
+                value_and_product(s, 1, woven)
             closed = []
             for g, j, nh, chunks in plan.get(s, []):
                 down_project(g, j, nh, chunks)

@@ -40,17 +40,15 @@ FLOPS = 2 * BATCH * GROUPS * (2 * RIN * HID + HID * DOUT)
 
 def mx_plan():
     plan = {}
-    for g in range(GROUPS):
-        for c in range(CHUNKS):
-            for j in range(B_TILES):
-                for nh in range(N_HALVES):
-                    if g < GROUPS - 1:
-                        if c == 0:
-                            plan.setdefault(CHUNKS * (g + 1) + j, []).append((g, j, nh, list(range(CHUNKS))))
-                    else:
-                        k = CHUNKS * g + c
-                        step = max(k + 1, min(k + 2, N_CHUNKS - 1))
-                        plan.setdefault(step, []).append((g, j, nh, [c]))
+    halves = range(N_HALVES)
+    for g in range(GROUPS - 1):
+        for j in range(B_TILES):
+            for nh in halves:
+                step = CHUNKS * (g + 1) + j
+                plan.setdefault(step, []).append((g, j, nh, list(range(CHUNKS))))
+    plan[N_CHUNKS] = [(GROUPS - 1, 0, nh, list(range(CHUNKS - 1))) for nh in halves]
+    plan[N_CHUNKS].extend((GROUPS - 1, 0, nh, [CHUNKS - 1]) for nh in halves)
+    plan[N_CHUNKS].extend((GROUPS - 1, j, nh, list(range(CHUNKS))) for j in range(1, B_TILES) for nh in halves)
     return plan
 
 
@@ -66,7 +64,7 @@ def tile_observationembeddingv2_pb_e_kernel(
         h_pool = ctx.enter_context(tc.tile_pool(name="h", bufs=4))
         q_pool = ctx.enter_context(tc.tile_pool(name="q", bufs=8))
         s_pool = ctx.enter_context(tc.tile_pool(name="s", bufs=4))
-        e_pool = ctx.enter_context(tc.tile_pool(name="e", bufs=4))
+        e_pool = ctx.enter_context(tc.tile_pool(name="e", bufs=6))
         psum = ctx.enter_context(tc.psum_pool(name="psum", bufs=8))
         ctx.enter_context(tc.manual_schedule())
 
@@ -103,12 +101,14 @@ def tile_observationembeddingv2_pb_e_kernel(
         w2_words = {}
         weights_t = {}
         wt_ps = {}
+        xt_ps = {}
         codes = {}
         planes = {}
         grouped = {}
         silu_sb = {}
         tok = {}
         sumsq = {}
+        first_eps = {}
         rstd = {}
         scaled = {}
 
@@ -152,15 +152,16 @@ def tile_observationembeddingv2_pb_e_kernel(
                 )
                 copy(out=dest[:, cols], in_=spread_ps[:])
 
-        def transpose_x(g):
-            xt_ps = psum.tile([P, B_TILES, P], F32, name="xt_ps", tag="bank")
+        def transpose_x_one(g, j):
+            if j == 0:
+                xt_ps[g] = psum.tile([P, B_TILES, P], F32, name="xt_ps", tag="bank")
             x_words = (x_first if g == 0 else x_rest)[:].bitcast(F32)
-            for j in range(B_TILES):
-                nc.tensor.transpose(xt_ps[:, j, :], x_words[:, j, max(g - 1, 0), :], ident[:])
-            nc.scalar.copy(
-                out=xT[:, g],
-                in_=xt_ps[:].rearrange("q j b -> q (j b)").bitcast(BF16).rearrange("q (b e) -> q e b", e=2),
-            )
+            nc.tensor.transpose(xt_ps[g][:, j, :], x_words[:, j, max(g - 1, 0), :], ident[:])
+            if j == B_TILES - 1:
+                nc.scalar.copy(
+                    out=xT[:, g],
+                    in_=xt_ps[g][:].rearrange("q j b -> q (j b)").bitcast(BF16).rearrange("q (b e) -> q e b", e=2),
+                )
 
         def transpose_one(k, i, t):
             if i == 0 and t == 0:
@@ -174,7 +175,7 @@ def tile_observationembeddingv2_pb_e_kernel(
                     load_chunk(k + RAW_BUFS)
 
         def chunk_transposes(k):
-            return [(k, i, t) for i in range(2) for t in range(PACK)]
+            return [(transpose_one, (k, i, t)) for i in range(2) for t in range(PACK)]
 
         def project(k, half, i, woven):
             g = k // CHUNKS
@@ -192,8 +193,8 @@ def tile_observationembeddingv2_pb_e_kernel(
                     m = ((i * HALVES + half) * T_HALF + tl) * 2 + e
                     first = (m * len(woven) + M_STEP - 1) // M_STEP
                     behind = ((m + 1) * len(woven) + M_STEP - 1) // M_STEP
-                    for task in woven[first:behind]:
-                        transpose_one(*task)
+                    for call, args in woven[first:behind]:
+                        call(*args)
             return acc
 
         def gate(k, half, woven):
@@ -240,7 +241,7 @@ def tile_observationembeddingv2_pb_e_kernel(
                 if j == B_TILES - 1 and nh == N_HALVES - 1 and k + W2_BUFS < N_CHUNKS:
                     load_w2(k + W2_BUFS)
 
-        def sum_squares(j, nh):
+        def sum_squares(j, nh, on_scalar):
             if nh == 0:
                 sumsq[j] = s_pool.tile([P, N_HALVES], F32, name="sumsq")
             squares = s_pool.tile([P, BANK], BF16, name="squares")
@@ -250,6 +251,15 @@ def tile_observationembeddingv2_pb_e_kernel(
                 func=ACT.Square,
                 scale=DOUT ** -0.5,
                 accum_out=sumsq[j][:, nh : nh + 1],
+            )
+            if nh == 0 and on_scalar:
+                first_eps[j] = s_pool.tile([P, 1], F32, name="first_eps")
+                nc.scalar.activation(out=first_eps[j][:], in_=sumsq[j][:, 0:1], func=ACT.Copy, bias=EPS)
+
+        def inverse_rms_scalar(j):
+            rstd[j] = s_pool.tile([P, 1], F32, name="rstd")
+            nc.scalar.activation(
+                out=rstd[j][:], in_=sumsq[j][:, 1:2], func=ACT.Abs_reciprocal_sqrt, bias=first_eps[j][:, 0:1]
             )
 
         def inverse_rms(j):
@@ -269,14 +279,22 @@ def tile_observationembeddingv2_pb_e_kernel(
         def normalise_and_store(g, j, nh):
             cols = slice(nh * BANK, (nh + 1) * BANK)
             result = e_pool.tile([P, BANK], F32, name="result")
-            nc.vector.scalar_tensor_tensor(
-                out=result[:],
-                in0=scaled[j, nh][:],
-                scalar=rstd[j][:, 0:1],
-                in1=bias[:, g, cols],
-                op0=ALU.mult,
-                op1=ALU.add,
-            )
+            if g == GROUPS - 1:
+                nc.vector.scalar_tensor_tensor(
+                    out=result[:],
+                    in0=scaled[j, nh][:],
+                    scalar=rstd[j][:, 0:1],
+                    in1=bias[:, g, cols],
+                    op0=ALU.mult,
+                    op1=ALU.add,
+                )
+            else:
+                normed = e_pool.tile([P, BANK], F32, name="normed")
+                nc.gpsimd.tensor_scalar(
+                    out=normed[:], in0=scaled[j, nh][:], scalar1=rstd[j][:, 0:1], scalar2=0.0,
+                    op0=ALU.mult, op1=ALU.add,
+                )
+                nc.gpsimd.tensor_tensor(out=result[:], in0=normed[:], in1=bias[:, g, cols], op=ALU.add)
             nc.sync.dma_start(out=out[j * P : (j + 1) * P, g, cols], in_=result[:])
 
         nc.sync.dma_start(out=x_first[:], in_=x_dram[:, :, 0:1, :])
@@ -291,9 +309,10 @@ def tile_observationembeddingv2_pb_e_kernel(
             if k + CHUNKS < RAW_BUFS:
                 load_chunk(k + CHUNKS)
 
-        transpose_x(0)
-        for task in chunk_transposes(0):
-            transpose_one(*task)
+        for j in range(B_TILES):
+            transpose_x_one(0, j)
+        for call, args in chunk_transposes(0):
+            call(*args)
 
         plan = mx_plan()
         closed = []
@@ -306,6 +325,8 @@ def tile_observationembeddingv2_pb_e_kernel(
             if live:
                 gate(s, 0, woven)
                 gate(s, 1, woven)
+            if s == N_CHUNKS - 1:
+                nc.scalar.activation(out=warm[:], in_=neg_half[:], func=ACT.Abs_reciprocal_sqrt)
             if 0 < s <= N_CHUNKS:
                 quantise(s - 1)
             for g, j in closed:
@@ -318,14 +339,23 @@ def tile_observationembeddingv2_pb_e_kernel(
             for g, j, nh, chunks in plan.get(s, []):
                 down_project(g, j, nh, chunks)
                 if CHUNKS - 1 in chunks:
-                    sum_squares(j, nh)
+                    sum_squares(j, nh, not live)
                     apply_gain(j, nh)
+                    if not live:
+                        for g_done, j_done in closed:
+                            for nh_done in range(N_HALVES):
+                                normalise_and_store(g_done, j_done, nh_done)
+                        closed = []
                     if nh == N_HALVES - 1:
-                        inverse_rms(j)
+                        if live:
+                            inverse_rms(j)
+                        else:
+                            inverse_rms_scalar(j)
                         closed.append((g, j))
             if s == 0:
                 spread_row(ident_bf[:, 0:1], gain[:], nc.scalar.copy)
             if live and c_now == 1:
                 spread_row(pick_bias[:, g_now : g_now + 1], bias[:, g_now, :], nc.scalar.copy)
             if live and c_now == 2 and g_now + 1 < GROUPS:
-                transpose_x(g_now + 1)
+                for j in range(B_TILES):
+                    transpose_x_one(g_now + 1, j)

@@ -31,7 +31,7 @@ BANK = 512
 N_HALVES = DOUT // BANK
 
 AHEAD = 2
-M_STEP = 16
+M_PHASE = 8
 RAW_BUFS = 8
 W2_BUFS = 8
 
@@ -152,49 +152,55 @@ def tile_observationembeddingv2_pb_e_kernel(
                 )
                 copy(out=dest[:, cols], in_=spread_ps[:])
 
-        def transpose_x_one(g, j):
-            if j == 0:
-                xt_ps[g] = psum.tile([P, B_TILES, P], F32, name="xt_ps", tag="bank")
-            x_words = (x_first if g == 0 else x_rest)[:].bitcast(F32)
-            nc.tensor.transpose(xt_ps[g][:, j, :], x_words[:, j, max(g - 1, 0), :], ident[:])
-            if j == B_TILES - 1:
-                nc.scalar.copy(
-                    out=xT[:, g],
-                    in_=xt_ps[g][:].rearrange("q j b -> q (j b)").bitcast(BF16).rearrange("q (b e) -> q e b", e=2),
-                )
+        def transpose_x_one(g, j, e):
+            if j == 0 and e == 0:
+                xt_ps[g] = psum.tile([P, 2, BATCH], BF16, name="xt_ps", tag="bank")
+            x_sb = x_first if g == 0 else x_rest
+            nc.tensor.transpose(
+                xt_ps[g][:, e, j * P : (j + 1) * P], x_sb[:, j, max(g - 1, 0), e * P : (e + 1) * P], ident_bf[:]
+            )
+            if j == B_TILES - 1 and e == 1:
+                nc.scalar.copy(out=xT[:, g], in_=xt_ps[g][:])
 
-        def transpose_one(k, i, t):
-            if i == 0 and t == 0:
-                weights_t[k] = wt_pool.tile([P, 2, PACK, P], F32, name="weights_t")
-            if t == 0:
-                wt_ps[k, i] = psum.tile([P, PACK, P], F32, name="wt_ps", tag="bank")
-            nc.tensor.transpose(wt_ps[k, i][:, t, :], raw[k][:].bitcast(F32)[:, i, t, :], ident[:])
-            if t == PACK - 1:
+        def x_transposes(g):
+            return [(transpose_x_one, (g, j, e)) for j in range(B_TILES) for e in range(2)]
+
+        def transpose_one(k, i, t, e):
+            if i == 0 and t == 0 and e == 0:
+                weights_t[k] = wt_pool.tile([P, 2, PACK, 2, P], BF16, name="weights_t")
+            if t == 0 and e == 0:
+                wt_ps[k, i] = psum.tile([P, PACK, 2, P], BF16, name="wt_ps", tag="bank")
+            nc.tensor.transpose(wt_ps[k, i][:, t, e, :], raw[k][:, i, t, e * P : (e + 1) * P], ident_bf[:])
+            if t == PACK - 1 and e == 1:
                 nc.scalar.copy(out=weights_t[k][:, i], in_=wt_ps[k, i][:])
                 if i == 1 and k + RAW_BUFS < N_CHUNKS:
                     load_chunk(k + RAW_BUFS)
 
         def chunk_transposes(k):
-            return [(transpose_one, (k, i, t)) for i in range(2) for t in range(PACK)]
+            return [(transpose_one, (k, i, t, e)) for i in range(2) for t in range(PACK) for e in range(2)]
 
         def project(k, half, i, woven):
             g = k // CHUNKS
-            pairs = weights_t[k][:].bitcast(BF16).rearrange("q i t (m e) -> q i t m e", e=2)
+            share = woven[: len(woven) // 2] if i == 0 else woven[len(woven) // 2 :]
             acc = psum.tile([P, T_HALF, BATCH], F32, name="acc", tag="bank")
             for tl in range(T_HALF):
                 for e in range(2):
+                    m = (half * T_HALF + tl) * 2 + e
+                    if i == 1:
+                        for call, args in share[m * len(share) // M_PHASE : (m + 1) * len(share) // M_PHASE]:
+                            call(*args)
                     nc.tensor.matmul(
                         out=acc[:, tl, :],
-                        lhsT=pairs[:, i, half * T_HALF + tl, :, e],
+                        lhsT=weights_t[k][:, i, half * T_HALF + tl, e, :],
                         rhs=xT[:, g, e, :],
                         start=(e == 0),
                         stop=(e == 1),
                     )
-                    m = ((i * HALVES + half) * T_HALF + tl) * 2 + e
-                    first = (m * len(woven) + M_STEP - 1) // M_STEP
-                    behind = ((m + 1) * len(woven) + M_STEP - 1) // M_STEP
-                    for call, args in woven[first:behind]:
-                        call(*args)
+                    if i == 0:
+                        first = (m * len(share) + M_PHASE - 1) // M_PHASE
+                        behind = ((m + 1) * len(share) + M_PHASE - 1) // M_PHASE
+                        for call, args in share[first:behind]:
+                            call(*args)
             return acc
 
         def gate(k, half, woven):
@@ -309,9 +315,7 @@ def tile_observationembeddingv2_pb_e_kernel(
             if k + CHUNKS < RAW_BUFS:
                 load_chunk(k + CHUNKS)
 
-        for j in range(B_TILES):
-            transpose_x_one(0, j)
-        for call, args in chunk_transposes(0):
+        for call, args in x_transposes(0) + chunk_transposes(0):
             call(*args)
 
         plan = mx_plan()
@@ -357,5 +361,5 @@ def tile_observationembeddingv2_pb_e_kernel(
             if live and c_now == 1:
                 spread_row(pick_bias[:, g_now : g_now + 1], bias[:, g_now, :], nc.scalar.copy)
             if live and c_now == 2 and g_now + 1 < GROUPS:
-                for j in range(B_TILES):
-                    transpose_x_one(g_now + 1, j)
+                for call, args in x_transposes(g_now + 1):
+                    call(*args)

@@ -44,7 +44,7 @@ def mx_plan():
     for g in range(GROUPS - 1):
         for j in range(B_TILES):
             for nh in halves:
-                step = CHUNKS * (g + 1) + j
+                step = CHUNKS * (g + 1) + (N_HALVES * j + nh if g < GROUPS - 2 else j)
                 plan.setdefault(step, []).append((g, j, nh, list(range(CHUNKS))))
     plan[N_CHUNKS] = [(GROUPS - 1, 0, nh, list(range(CHUNKS - 1))) for nh in halves]
     plan[N_CHUNKS].extend((GROUPS - 1, 0, nh, [CHUNKS - 1]) for nh in halves)
@@ -310,10 +310,9 @@ def tile_observationembeddingv2_pb_e_kernel(
         nc.sync.dma_start(out=rows[1:2, :], in_=norm_b.unsqueeze(0))
         nc.sync.dma_start(out=rows[2 : 2 + GROUPS, :], in_=term_embed_r)
         nc.sync.dma_start(out=x_rest[:], in_=x_dram[:, :, 1:, :])
-        for k in range(W2_BUFS):
+        for k in range(CHUNKS):
             load_w2(k)
-            if k + CHUNKS < RAW_BUFS:
-                load_chunk(k + CHUNKS)
+            load_chunk(k + CHUNKS)
 
         for call, args in x_transposes(0) + chunk_transposes(0):
             call(*args)
@@ -326,6 +325,8 @@ def tile_observationembeddingv2_pb_e_kernel(
             woven = []
             for k in range(1 if s == 0 else s + AHEAD, min(s + AHEAD + 1, N_CHUNKS)):
                 woven.extend(chunk_transposes(k))
+            if live and c_now == 2 and g_now + 1 < GROUPS:
+                woven.extend(x_transposes(g_now + 1))
             if live:
                 gate(s, 0, woven)
                 gate(s, 1, woven)
@@ -360,6 +361,5 @@ def tile_observationembeddingv2_pb_e_kernel(
                 spread_row(ident_bf[:, 0:1], gain[:], nc.scalar.copy)
             if live and c_now == 1:
                 spread_row(pick_bias[:, g_now : g_now + 1], bias[:, g_now, :], nc.scalar.copy)
-            if live and c_now == 2 and g_now + 1 < GROUPS:
-                for call, args in x_transposes(g_now + 1):
-                    call(*args)
+            if s < CHUNKS:
+                load_w2(CHUNKS + s)

@@ -123,34 +123,47 @@ def tile_observationembeddingv2_pb_e_kernel(
                     ),
                 )
 
+        def load_scales(g):
+            for quad in range(4):
+                nc.sync.dma_start(
+                    out=w2_planes[32 * quad : 32 * quad + 16, g, :].bitcast(I32),
+                    in_=w2_r_scales[
+                        CHUNKS * g : CHUNKS * (g + 1), 4 * quad : 4 * quad + 4, :
+                    ].bitcast(I32),
+                )
+
         def load_w2(k):
             g, c = divmod(k, CHUNKS)
             if c == 0:
-                for quad in range(4):
-                    nc.sync.dma_start(
-                        out=w2_planes[32 * quad : 32 * quad + 16, g, :].bitcast(I32),
-                        in_=w2_r_scales[
-                            CHUNKS * g : CHUNKS * (g + 1), 4 * quad : 4 * quad + 4, :
-                        ].bitcast(I32),
-                    )
+                load_scales(g)
             w2_words[k] = w2_pool.tile([P, DOUT], U32, name="w2_words", align_bytes=64)
             nc.sync.dma_start(
                 out=w2_words[k][:].bitcast(I32),
                 in_=w2_r_words[k].rearrange("p n t -> p (n t)").bitcast(I32),
             )
 
-        def spread_row(pick, dest, copy):
-            for nh in range(N_HALVES):
-                cols = slice(nh * BANK, (nh + 1) * BANK)
-                spread_ps = psum.tile([P, BANK], F32, name="spread_ps", tag="bank")
-                nc.tensor.matmul(
-                    out=spread_ps[:],
-                    lhsT=pick.to_broadcast([P, P]),
-                    rhs=rows[:, cols],
-                    start=True,
-                    stop=True,
+        def load_first_w2(nh):
+            for k in range(CHUNKS):
+                if nh == 0:
+                    w2_words[k] = w2_pool.tile([P, DOUT], U32, name="w2_words", align_bytes=64)
+                nc.sync.dma_start(
+                    out=w2_words[k][:, nh * BANK : (nh + 1) * BANK].bitcast(I32),
+                    in_=w2_r_words[k].rearrange("p n t -> p (n t)")[
+                        :, nh * BANK * PACK : (nh + 1) * BANK * PACK
+                    ].bitcast(I32),
                 )
-                copy(out=dest[:, cols], in_=spread_ps[:])
+
+        def spread_row(pick, dest, nh):
+            cols = slice(nh * BANK, (nh + 1) * BANK)
+            spread_ps = psum.tile([P, BANK], F32, name="spread_ps", tag="bank")
+            nc.tensor.matmul(
+                out=spread_ps[:],
+                lhsT=pick.to_broadcast([P, P]),
+                rhs=rows[:, cols],
+                start=True,
+                stop=True,
+            )
+            nc.vector.tensor_copy(out=dest[:, cols], in_=spread_ps[:])
 
         def transpose_x_one(g, j, e):
             if j == 0 and e == 0:
@@ -309,10 +322,14 @@ def tile_observationembeddingv2_pb_e_kernel(
         nc.sync.dma_start(out=rows[0:1, :], in_=norm_w.unsqueeze(0))
         nc.sync.dma_start(out=rows[1:2, :], in_=norm_b.unsqueeze(0))
         nc.sync.dma_start(out=rows[2 : 2 + GROUPS, :], in_=term_embed_r)
+        load_chunk(4)
         nc.sync.dma_start(out=x_rest[:], in_=x_dram[:, :, 1:, :])
-        for k in range(CHUNKS):
-            load_w2(k)
-            load_chunk(k + CHUNKS)
+        load_chunk(5)
+        load_scales(0)
+        load_first_w2(0)
+        load_chunk(6)
+        load_chunk(7)
+        load_first_w2(1)
 
         for call, args in x_transposes(0) + chunk_transposes(0):
             call(*args)
@@ -357,9 +374,9 @@ def tile_observationembeddingv2_pb_e_kernel(
                         else:
                             inverse_rms_scalar(j)
                         closed.append((g, j))
-            if s == 0:
-                spread_row(ident_bf[:, 0:1], gain[:], nc.scalar.copy)
-            if live and c_now == 1:
-                spread_row(pick_bias[:, g_now : g_now + 1], bias[:, g_now, :], nc.scalar.copy)
+            if s == 0 or s == CHUNKS - 1:
+                spread_row(ident_bf[:, 0:1], gain[:], min(s, 1))
+            if live and 1 <= c_now <= N_HALVES:
+                spread_row(pick_bias[:, g_now : g_now + 1], bias[:, g_now, :], c_now - 1)
             if s < CHUNKS:
                 load_w2(CHUNKS + s)

@@ -34,6 +34,7 @@ AHEAD = 2
 M_PHASE = 8
 RAW_BUFS = 8
 W2_BUFS = 8
+WARM_UP = 3
 
 FLOPS = 2 * BATCH * GROUPS * (2 * RIN * HID + HID * DOUT)
 
@@ -72,16 +73,26 @@ def tile_observationembeddingv2_pb_e_kernel(
         nc.gpsimd.memset(neg_half[:], -0.5)
         warm = const.tile([P, 1], F32, name="warm")
         nc.scalar.activation(out=warm[:], in_=neg_half[:], func=ACT.Silu)
-        ident = const.tile([P, P], F32, name="ident")
-        make_identity(nc, ident[:])
+        ident_bf = const.tile([P, P], BF16, name="ident_bf")
+        make_identity(nc, ident_bf[:])
+
+        zeros = const.tile([P, BANK], BF16, name="zeros")
+        nc.vector.memset(zeros[:], 0.0)
+        idle_ps = psum.tile([P, BANK], F32, name="idle_ps", tag="bank")
+
+        def idle_matmul(width):
+            nc.tensor.matmul(
+                out=idle_ps[:, 0:width], lhsT=zeros[:, 0:P], rhs=zeros[:, 0:width], start=True, stop=True
+            )
+
+        for n in range(WARM_UP):
+            idle_matmul(BANK)
 
         rows = const.tile([P, DOUT], BF16, name="rows")
         nc.vector.memset(rows[:], 0.0)
         w2_planes = const.tile([P, GROUPS, DOUT], U8, name="w2_planes", align_bytes=64)
         nc.vector.memset(w2_planes[:].bitcast(I32), 0)
 
-        ident_bf = const.tile([P, P], BF16, name="ident_bf")
-        nc.vector.tensor_copy(out=ident_bf[:], in_=ident[:])
         pick_bias = const.tile([P, GROUPS], BF16, name="pick_bias")
         nc.vector.tensor_tensor(
             out=pick_bias[:],
@@ -89,6 +100,10 @@ def tile_observationembeddingv2_pb_e_kernel(
             in1=ident_bf[:, 2 : 2 + GROUPS],
             op=ALU.add,
         )
+        pick_tiles = const.tile([P, 1 + GROUPS, P], BF16, name="pick_tiles")
+        nc.vector.tensor_copy(out=pick_tiles[:, 0, :], in_=ident_bf[:, 0:1].to_broadcast([P, P]))
+        for g in range(GROUPS):
+            nc.vector.tensor_copy(out=pick_tiles[:, 1 + g, :], in_=pick_bias[:, g : g + 1].to_broadcast([P, P]))
 
         x_first = const.tile([P, B_TILES, 1, RIN], BF16, name="x_first")
         x_rest = const.tile([P, B_TILES, GROUPS - 1, RIN], BF16, name="x_rest")
@@ -158,7 +173,7 @@ def tile_observationembeddingv2_pb_e_kernel(
             spread_ps = psum.tile([P, BANK], F32, name="spread_ps", tag="bank")
             nc.tensor.matmul(
                 out=spread_ps[:],
-                lhsT=pick.to_broadcast([P, P]),
+                lhsT=pick,
                 rhs=rows[:, cols],
                 start=True,
                 stop=True,
@@ -331,8 +346,13 @@ def tile_observationembeddingv2_pb_e_kernel(
         load_chunk(7)
         load_first_w2(1)
 
-        for call, args in x_transposes(0) + chunk_transposes(0):
+        for call, args in x_transposes(0):
             call(*args)
+        first = chunk_transposes(0)
+        for part in (first[: len(first) // 2], first[len(first) // 2 :]):
+            idle_matmul(BATCH)
+            for call, args in part:
+                call(*args)
 
         plan = mx_plan()
         closed = []
@@ -375,8 +395,8 @@ def tile_observationembeddingv2_pb_e_kernel(
                             inverse_rms_scalar(j)
                         closed.append((g, j))
             if s == 0 or s == CHUNKS - 1:
-                spread_row(ident_bf[:, 0:1], gain[:], min(s, 1))
+                spread_row(pick_tiles[:, 0, :], gain[:], min(s, 1))
             if live and 1 <= c_now <= N_HALVES:
-                spread_row(pick_bias[:, g_now : g_now + 1], bias[:, g_now, :], c_now - 1)
+                spread_row(pick_tiles[:, 1 + g_now, :], bias[:, g_now, :], c_now - 1)
             if s < CHUNKS:
                 load_w2(CHUNKS + s)

from contextlib import ExitStack

import concourse.mybir as mybir
from concourse.masks import make_identity

F32 = mybir.dt.float32
BF16 = mybir.dt.bfloat16
I32 = mybir.dt.int32
U32 = mybir.dt.uint32
U8 = mybir.dt.uint8
FP8X4 = mybir.dt.float8_e4m3fn_x4
ACT = mybir.ActivationFunctionType
ALU = mybir.AluOpType

P = 128
PACK = 4
BATCH = 256
GROUPS = 5
RIN = 256
HID = 2048
DOUT = 1024
EPS = 1e-05

K_PASS = P * PACK
CHUNKS = HID // K_PASS
N_CHUNKS = GROUPS * CHUNKS
HALVES = 2
T_HALF = PACK // HALVES
B_TILES = BATCH // P
BANK = 512
N_HALVES = DOUT // BANK

AHEAD = 2
M_PHASE = 8
RAW_BUFS = 8
W2_BUFS = 8
WARM_UP = 3

FLOPS = 2 * BATCH * GROUPS * (2 * RIN * HID + HID * DOUT)


def mx_plan():
    plan = {}
    halves = range(N_HALVES)
    for g in range(GROUPS - 1):
        for j in range(B_TILES):
            for nh in halves:
                step = CHUNKS * (g + 1) + (N_HALVES * j + nh if g < GROUPS - 2 else j)
                plan.setdefault(step, []).append((g, j, nh, list(range(CHUNKS))))
    plan[N_CHUNKS] = [(GROUPS - 1, 0, nh, list(range(CHUNKS - 1))) for nh in halves]
    plan[N_CHUNKS].extend((GROUPS - 1, 0, nh, [CHUNKS - 1]) for nh in halves)
    plan[N_CHUNKS].extend((GROUPS - 1, j, nh, list(range(CHUNKS))) for j in range(1, B_TILES) for nh in halves)
    return plan


def tile_observationembeddingv2_pb_e_kernel(
    tc, xr, w1_r, w3_r, w2_r_words, w2_r_scales, norm_w, norm_b, term_embed_r, out
):
    nc = tc.nc
    with ExitStack() as ctx:
        const = ctx.enter_context(tc.tile_pool(name="const", bufs=1))
        raw_pool = ctx.enter_context(tc.tile_pool(name="raw", bufs=RAW_BUFS))
        w2_pool = ctx.enter_context(tc.tile_pool(name="w2", bufs=W2_BUFS))
        wt_pool = ctx.enter_context(tc.tile_pool(name="wt", bufs=AHEAD + 2))
        h_pool = ctx.enter_context(tc.tile_pool(name="h", bufs=4))
        q_pool = ctx.enter_context(tc.tile_pool(name="q", bufs=8))
        s_pool = ctx.enter_context(tc.tile_pool(name="s", bufs=4))
        e_pool = ctx.enter_context(tc.tile_pool(name="e", bufs=6))
        psum = ctx.enter_context(tc.psum_pool(name="psum", bufs=8))
        ctx.enter_context(tc.manual_schedule())

        neg_half = const.tile([P, 1], F32, name="neg_half")
        nc.gpsimd.memset(neg_half[:], -0.5)
        warm = const.tile([P, 1], F32, name="warm")
        nc.scalar.activation(out=warm[:], in_=neg_half[:], func=ACT.Silu)
        ident_bf = const.tile([P, P], BF16, name="ident_bf")
        make_identity(nc, ident_bf[:])

        zeros = const.tile([P, BANK], BF16, name="zeros")
        nc.vector.memset(zeros[:], 0.0)
        idle_ps = psum.tile([P, BANK], F32, name="idle_ps", tag="bank")

        def idle_matmul(width):
            nc.tensor.matmul(
                out=idle_ps[:, 0:width], lhsT=zeros[:, 0:P], rhs=zeros[:, 0:width], start=True, stop=True
            )

        for n in range(WARM_UP):
            idle_matmul(BANK)

        rows = const.tile([P, DOUT], BF16, name="rows")
        nc.vector.memset(rows[:], 0.0)
        w2_planes = const.tile([P, GROUPS, DOUT], U8, name="w2_planes", align_bytes=64)
        nc.vector.memset(w2_planes[:].bitcast(I32), 0)

        pick_bias = const.tile([P, GROUPS], BF16, name="pick_bias")
        nc.vector.tensor_tensor(
            out=pick_bias[:],
            in0=ident_bf[:, 1:2].to_broadcast([P, GROUPS]),
            in1=ident_bf[:, 2 : 2 + GROUPS],
            op=ALU.add,
        )
        pick_tiles = const.tile([P, 1 + GROUPS, P], BF16, name="pick_tiles")
        nc.vector.tensor_copy(out=pick_tiles[:, 0, :], in_=ident_bf[:, 0:1].to_broadcast([P, P]))
        for g in range(GROUPS):
            nc.vector.tensor_copy(out=pick_tiles[:, 1 + g, :], in_=pick_bias[:, g : g + 1].to_broadcast([P, P]))

        x_first = const.tile([P, B_TILES, 1, RIN], BF16, name="x_first")
        x_rest = const.tile([P, B_TILES, GROUPS - 1, RIN], BF16, name="x_rest")
        x_dram = xr.rearrange("(j p) g k -> p j g k", p=P)
        xT = const.tile([P, GROUPS, 2, BATCH], BF16, name="xT")
        gain = const.tile([P, DOUT], F32, name="gain")
        bias = const.tile([P, GROUPS, DOUT], F32, name="bias")

        raw = {}
        w2_words = {}
        weights_t = {}
        wt_ps = {}
        xt_ps = {}
        codes = {}
        planes = {}
        grouped = {}
        silu_sb = {}
        tok = {}
        sumsq = {}
        first_eps = {}
        rstd = {}
        scaled = {}

        def load_chunk(k):
            g, c = divmod(k, CHUNKS)
            raw[k] = raw_pool.tile([P, 2, PACK, RIN], BF16, name="raw")
            for i, w in enumerate((w1_r, w3_r)):
                nc.sync.dma_start(
                    out=raw[k][:, i].rearrange("p t k -> p (t k)"),
                    in_=w[g, c * K_PASS : (c + 1) * K_PASS, :].rearrange(
                        "(p t) k -> p (t k)", t=PACK
                    ),
                )

        def load_scales(g):
            for quad in range(4):
                nc.sync.dma_start(
                    out=w2_planes[32 * quad : 32 * quad + 16, g, :].bitcast(I32),
                    in_=w2_r_scales[
                        CHUNKS * g : CHUNKS * (g + 1), 4 * quad : 4 * quad + 4, :
                    ].bitcast(I32),
                )

        def load_w2(k):
            g, c = divmod(k, CHUNKS)
            if c == 0:
                load_scales(g)
            w2_words[k] = w2_pool.tile([P, DOUT], U32, name="w2_words", align_bytes=64)
            nc.sync.dma_start(
                out=w2_words[k][:].bitcast(I32),
                in_=w2_r_words[k].rearrange("p n t -> p (n t)").bitcast(I32),
            )

        def load_first_w2(nh):
            for k in range(CHUNKS):
                if nh == 0:
                    w2_words[k] = w2_pool.tile([P, DOUT], U32, name="w2_words", align_bytes=64)
                nc.sync.dma_start(
                    out=w2_words[k][:, nh * BANK : (nh + 1) * BANK].bitcast(I32),
                    in_=w2_r_words[k].rearrange("p n t -> p (n t)")[
                        :, nh * BANK * PACK : (nh + 1) * BANK * PACK
                    ].bitcast(I32),
                )

        def spread_row(pick, dest, nh):
            cols = slice(nh * BANK, (nh + 1) * BANK)
            spread_ps = psum.tile([P, BANK], F32, name="spread_ps", tag="bank")
            nc.tensor.matmul(
                out=spread_ps[:],
                lhsT=pick,
                rhs=rows[:, cols],
                start=True,
                stop=True,
            )
            nc.vector.tensor_copy(out=dest[:, cols], in_=spread_ps[:])

        def transpose_x_one(g, j, e):
            if j == 0 and e == 0:
                xt_ps[g] = psum.tile([P, 2, BATCH], BF16, name="xt_ps", tag="bank")
            x_sb = x_first if g == 0 else x_rest
            nc.tensor.transpose(
                xt_ps[g][:, e, j * P : (j + 1) * P], x_sb[:, j, max(g - 1, 0), e * P : (e + 1) * P], ident_bf[:]
            )
            if j == B_TILES - 1 and e == 1:
                nc.scalar.copy(out=xT[:, g], in_=xt_ps[g][:])

        def x_transposes(g):
            return [(transpose_x_one, (g, j, e)) for j in range(B_TILES) for e in range(2)]

        def transpose_one(k, i, t, e):
            if i == 0 and t == 0 and e == 0:
                weights_t[k] = wt_pool.tile([P, 2, PACK, 2, P], BF16, name="weights_t")
            if t == 0 and e == 0:
                wt_ps[k, i] = psum.tile([P, PACK, 2, P], BF16, name="wt_ps", tag="bank")
            nc.tensor.transpose(wt_ps[k, i][:, t, e, :], raw[k][:, i, t, e * P : (e + 1) * P], ident_bf[:])
            if t == PACK - 1 and e == 1:
                nc.scalar.copy(out=weights_t[k][:, i], in_=wt_ps[k, i][:])
                if i == 1 and k + RAW_BUFS < N_CHUNKS:
                    load_chunk(k + RAW_BUFS)

        def chunk_transposes(k):
            return [(transpose_one, (k, i, t, e)) for i in range(2) for t in range(PACK) for e in range(2)]

        def project(k, half, i, woven):
            g = k // CHUNKS
            share = woven[: len(woven) // 2] if i == 0 else woven[len(woven) // 2 :]
            acc = psum.tile([P, T_HALF, BATCH], F32, name="acc", tag="bank")
            for tl in range(T_HALF):
                for e in range(2):
                    m = (half * T_HALF + tl) * 2 + e
                    if i == 1:
                        for call, args in share[m * len(share) // M_PHASE : (m + 1) * len(share) // M_PHASE]:
                            call(*args)
                    nc.tensor.matmul(
                        out=acc[:, tl, :],
                        lhsT=weights_t[k][:, i, half * T_HALF + tl, e, :],
                        rhs=xT[:, g, e, :],
                        start=(e == 0),
                        stop=(e == 1),
                    )
                    if i == 0:
                        first = (m * len(share) + M_PHASE - 1) // M_PHASE
                        behind = ((m + 1) * len(share) + M_PHASE - 1) // M_PHASE
                        for call, args in share[first:behind]:
                            call(*args)
            return acc

        def gate(k, half, woven):
            gate_ps = project(k, half, 0, woven)
            silu_sb[k, half] = h_pool.tile([P, T_HALF, BATCH], F32, name="silu_sb")
            nc.scalar.activation(out=silu_sb[k, half][:], in_=gate_ps[:], func=ACT.Silu)

        def value_and_product(k, half, woven):
            value_ps = project(k, half, 1, woven)
            if half == 0:
                grouped[k] = h_pool.tile([P, BATCH, PACK], BF16, name="grouped", align_bytes=64)
            nc.vector.tensor_tensor(
                out=grouped[k][:, :, half * T_HALF : (half + 1) * T_HALF],
                in0=value_ps[:].rearrange("p t b -> p b t"),
                in1=silu_sb[k, half][:].rearrange("p t b -> p b t"),
                op=ALU.mult,
            )

        def quantise(k):
            codes[k] = q_pool.tile([P, BATCH], U32, name="codes", align_bytes=64)
            planes[k] = q_pool.tile([P, BATCH], U8, name="planes", align_bytes=64)
            nc.vector.quantize_mx(
                out=codes[k][:].bitcast(FP8X4),
                scales=planes[k][:],
                in_=grouped[k][:].rearrange("p b t -> p (b t)"),
            )

        def down_project(g, j, nh, chunks):
            rows_b = slice(j * P, (j + 1) * P)
            cols = slice(nh * BANK, (nh + 1) * BANK)
            for c in chunks:
                k = CHUNKS * g + c
                if c == 0:
                    tok[j, nh] = psum.tile([P, BANK], F32, name="tok", tag="bank")
                nc.tensor.matmul_mx(
                    out=tok[j, nh][:],
                    lhsT=codes[k][:, rows_b].bitcast(FP8X4),
                    lhsT_scale=planes[k][:, rows_b],
                    rhs=w2_words[k][:, cols].bitcast(FP8X4),
                    rhs_scale=w2_planes[4 * c : P, g, cols],
                    start=(c == 0),
                    stop=(c == CHUNKS - 1),
                )
                if j == B_TILES - 1 and nh == N_HALVES - 1 and k + W2_BUFS < N_CHUNKS:
                    load_w2(k + W2_BUFS)

        def sum_squares(j, nh, on_scalar):
            if nh == 0:
                sumsq[j] = s_pool.tile([P, N_HALVES], F32, name="sumsq")
            squares = s_pool.tile([P, BANK], BF16, name="squares")
            nc.scalar.activation(
                out=squares[:],
                in_=tok[j, nh][:],
                func=ACT.Square,
                scale=DOUT ** -0.5,
                accum_out=sumsq[j][:, nh : nh + 1],
            )
            if nh == 0 and on_scalar:
                first_eps[j] = s_pool.tile([P, 1], F32, name="first_eps")
                nc.scalar.activation(out=first_eps[j][:], in_=sumsq[j][:, 0:1], func=ACT.Copy, bias=EPS)

        def inverse_rms_scalar(j):
            rstd[j] = s_pool.tile([P, 1], F32, name="rstd")
            nc.scalar.activation(
                out=rstd[j][:], in_=sumsq[j][:, 1:2], func=ACT.Abs_reciprocal_sqrt, bias=first_eps[j][:, 0:1]
            )

        def inverse_rms(j):
            mean_eps = s_pool.tile([P, 1], F32, name="mean_eps")
            nc.gpsimd.tensor_scalar(
                out=mean_eps[:], in0=sumsq[j][:, 0:1], scalar1=sumsq[j][:, 1:2], scalar2=EPS,
                op0=ALU.add, op1=ALU.add,
            )
            rstd[j] = s_pool.tile([P, 1], F32, name="rstd")
            nc.gpsimd.tensor_tensor(out=rstd[j][:], in0=mean_eps[:], in1=neg_half[:], op=ALU.pow)

        def apply_gain(j, nh):
            cols = slice(nh * BANK, (nh + 1) * BANK)
            scaled[j, nh] = e_pool.tile([P, BANK], F32, name="scaled")
            nc.vector.tensor_tensor(out=scaled[j, nh][:], in0=tok[j, nh][:], in1=gain[:, cols], op=ALU.mult)

        def normalise_and_store(g, j, nh):
            cols = slice(nh * BANK, (nh + 1) * BANK)
            result = e_pool.tile([P, BANK], F32, name="result")
            if g == GROUPS - 1:
                nc.vector.scalar_tensor_tensor(
                    out=result[:],
                    in0=scaled[j, nh][:],
                    scalar=rstd[j][:, 0:1],
                    in1=bias[:, g, cols],
                    op0=ALU.mult,
                    op1=ALU.add,
                )
            else:
                normed = e_pool.tile([P, BANK], F32, name="normed")
                nc.gpsimd.tensor_scalar(
                    out=normed[:], in0=scaled[j, nh][:], scalar1=rstd[j][:, 0:1], scalar2=0.0,
                    op0=ALU.mult, op1=ALU.add,
                )
                nc.gpsimd.tensor_tensor(out=result[:], in0=normed[:], in1=bias[:, g, cols], op=ALU.add)
            nc.sync.dma_start(out=out[j * P : (j + 1) * P, g, cols], in_=result[:])

        nc.sync.dma_start(out=x_first[:], in_=x_dram[:, :, 0:1, :])
        for k in range(CHUNKS):
            load_chunk(k)
        nc.sync.dma_start(out=rows[0:1, :], in_=norm_w.unsqueeze(0))
        nc.sync.dma_start(out=rows[1:2, :], in_=norm_b.unsqueeze(0))
        nc.sync.dma_start(out=rows[2 : 2 + GROUPS, :], in_=term_embed_r)
        load_chunk(4)
        nc.sync.dma_start(out=x_rest[:], in_=x_dram[:, :, 1:, :])
        load_chunk(5)
        load_scales(0)
        load_first_w2(0)
        load_chunk(6)
        load_chunk(7)
        load_first_w2(1)

        for call, args in x_transposes(0):
            call(*args)
        first = chunk_transposes(0)
        for part in (first[: len(first) // 2], first[len(first) // 2 :]):
            idle_matmul(BATCH)
            for call, args in part:
                call(*args)

        plan = mx_plan()
        closed = []
        for s in range(max(plan) + 2):
            g_now, c_now = divmod(s, CHUNKS)
            live = s < N_CHUNKS
            woven = []
            for k in range(1 if s == 0 else s + AHEAD, min(s + AHEAD + 1, N_CHUNKS)):
                woven.extend(chunk_transposes(k))
            if live and c_now == 2 and g_now + 1 < GROUPS:
                woven.extend(x_transposes(g_now + 1))
            if live:
                gate(s, 0, woven)
                gate(s, 1, woven)
            if s == N_CHUNKS - 1:
                nc.scalar.activation(out=warm[:], in_=neg_half[:], func=ACT.Abs_reciprocal_sqrt)
            if 0 < s <= N_CHUNKS:
                quantise(s - 1)
            for g, j in closed:
                for nh in range(N_HALVES):
                    normalise_and_store(g, j, nh)
            if live:
                value_and_product(s, 0, woven)
                value_and_product(s, 1, woven)
            closed = []
            for g, j, nh, chunks in plan.get(s, []):
                down_project(g, j, nh, chunks)
                if CHUNKS - 1 in chunks:
                    sum_squares(j, nh, not live)
                    apply_gain(j, nh)
                    if not live:
                        for g_done, j_done in closed:
                            for nh_done in range(N_HALVES):
                                normalise_and_store(g_done, j_done, nh_done)
                        closed = []
                    if nh == N_HALVES - 1:
                        if live:
                            inverse_rms(j)
                        else:
                            inverse_rms_scalar(j)
                        closed.append((g, j))
            if s == 0 or s == CHUNKS - 1:
                spread_row(pick_tiles[:, 0, :], gain[:], min(s, 1))
            if live and 1 <= c_now <= N_HALVES:
                spread_row(pick_tiles[:, 1 + g_now, :], bias[:, g_now, :], c_now - 1)
            if s < CHUNKS:
                load_w2(CHUNKS + s)
